import numpy as np
import ml_dtypes


def mxq(x, axis, fmt="e4m3"):
    dtype, down = {"e4m3": (ml_dtypes.float8_e4m3fn, 7), "e5m2": (ml_dtypes.float8_e5m2, 14)}[fmt]
    v = np.moveaxis(np.asarray(x, np.float32).astype(ml_dtypes.bfloat16).astype(np.float64), axis, -1)
    blocks = v.reshape(v.shape[:-1] + (-1, 32))
    amax = np.abs(blocks).max(-1, keepdims=True)
    byte = np.maximum(np.where(amax > 0, np.frexp(amax)[1] - 1 + 127, 0) - down, 1)
    scale = np.exp2(byte - 127.0)
    codes = (blocks / scale).astype(np.float32).astype(dtype).astype(np.float64)
    return np.moveaxis((codes * scale).reshape(v.shape), -1, axis)


WIDE = False


def mx_kscale(k):
    if not WIDE:
        return np.ones(k)
    levels = np.array([10, -10, 5, -5, 0])
    a = np.random.permutation(np.resize(levels, k // 512 * 4)).reshape(k // 512, 4)
    idx = np.arange(k)
    return np.exp2(a[idx // 512, idx % 128 // 32])


BF16 = ml_dtypes.bfloat16


def bf(x):
    return np.asarray(x, np.float32).astype(BF16)


def f64(x):
    return np.asarray(x).astype(np.float64)


T, B, C, E, H = 256, 16, 256, 512, 4
D = E // H
S = C + T
NEG_INF = -10000000000.0


def setup_inputs():
    s = mx_kscale(E)
    return {
        "x": bf(np.random.standard_normal((T, B, E)) * s),
        "q": bf(np.random.standard_normal((T, B, E)) * 2.0 / np.sqrt(D)),
        "k_new": bf(np.random.standard_normal((T, B, E))),
        "cache_k": bf(np.random.standard_normal((B * H, C, D))),
        "cache_v": bf(np.random.standard_normal((B * H, C, D))),
        "Wv": bf(np.random.standard_normal((E, E)) / np.sqrt(E) / s[None, :]),
        "bv": bf(np.random.standard_normal(E) * 0.3),
    }


def reference(x, q, k_new, cache_k, cache_v, Wv, bv):
    v_new = (mxq(f64(x), 2, "e4m3") @ mxq(f64(Wv), 1, "e4m3").T) + f64(bv)
    vh = v_new.reshape(T, B * H, D).transpose(1, 0, 2)
    qh = f64(q).reshape(T, B * H, D).transpose(1, 0, 2)
    kh = f64(k_new).reshape(T, B * H, D).transpose(1, 0, 2)
    causal = np.triu(np.full((T, T), NEG_INF), k=1)
    s_cache = qh @ f64(cache_k).transpose(0, 2, 1)
    s_new = qh @ kh.transpose(0, 2, 1)
    s = np.concatenate([s_cache, s_new + causal[None, :, :]], axis=2)
    e = np.exp(s - s.max(-1, keepdims=True))
    v = np.concatenate([f64(cache_v), vh], axis=1)
    attn = (mxq(e, 2, "e4m3") @ mxq(v, 1, "e4m3")) / e.sum(-1, keepdims=True)
    merged = attn.transpose(1, 0, 2).reshape(T, B, E)
    return merged, vh

@@ -1,0 +1,313 @@
+from contextlib import ExitStack
+
+import concourse.mybir as mybir
+from concourse.masks import make_identity
+
+F32 = mybir.dt.float32
+BF16 = mybir.dt.bfloat16
+U32 = mybir.dt.uint32
+U8 = mybir.dt.uint8
+FP8X4 = mybir.dt.float8_e4m3fn_x4
+ALU = mybir.AluOpType
+ACT = mybir.ActivationFunctionType
+AX = mybir.AxisListType
+
+T, B, C, E, H = 256, 16, 256, 512, 4
+D = 128
+P = 128
+NH = B * H
+FLOPS = 2 * T * B * E * E + 2 * 2 * NH * T * (C + T) * D
+
+MANUAL = False
+NG = 3
+CB = 2
+NCH = B // CB
+
+
+def tile_multiheadlmattentionwithcache_pa_t_kernel(
+    tc, x, q, k_new, cache_k, cache_v, Wv, bv, out_0, out_1
+):
+    nc = tc.nc
+    with ExitStack() as ctx:
+        const = ctx.enter_context(tc.tile_pool(name="const", bufs=1))
+        ld = ctx.enter_context(tc.tile_pool(name="ld", bufs=3))
+        w2 = ctx.enter_context(tc.tile_pool(name="w2", bufs=2))
+        w3 = ctx.enter_context(tc.tile_pool(name="w3", bufs=3))
+        w4 = ctx.enter_context(tc.tile_pool(name="w4", bufs=4))
+        ps_s = ctx.enter_context(tc.psum_pool(name="ps_s", bufs=3))
+        ps_e = ctx.enter_context(tc.psum_pool(name="ps_e", bufs=2))
+        ps_m = ctx.enter_context(tc.psum_pool(name="ps_m", bufs=3))
+
+        x_v = x.rearrange("(tt p) b e -> p tt (b e)", p=P)
+        q_v = q.rearrange("(tt p) b e -> p tt (b e)", p=P)
+        k_v = k_new.rearrange("(tt p) b e -> p tt (b e)", p=P)
+        ck_v = cache_k.rearrange("n (p j) d -> p n (j d)", j=2)
+        cv_v = cache_v.rearrange("n (p j) d -> p n (j d)", j=2)
+        o0_v = out_0.rearrange("(qt p) b e -> p qt b e", p=P)
+        o1_v = out_1.rearrange("(b h) (tt p) d -> p b tt h d", h=H, p=P)
+
+        chunks = {}
+        st = {}
+
+        def load_chunk(c):
+            w = CB * E
+            xs = ld.tile([P, 2 * w], BF16, name="xs", tag="xs")
+            qs = ld.tile([P, 2 * w], BF16, name="qs", tag="qs")
+            ks = ld.tile([P, 2 * w], BF16, name="ks", tag="ks")
+            cks = ld.tile([P, CB * H * 256], BF16, name="cks", tag="cks")
+            vst = ld.tile([P, CB * H, 4, D], BF16, name="vst", tag="vst")
+            nc.sync.dma_start(out=xs[:].rearrange("p (tt f) -> p tt f", tt=2), in_=x_v[:, :, c * w:(c + 1) * w])
+            nc.sync.dma_start(out=qs[:].rearrange("p (tt f) -> p tt f", tt=2), in_=q_v[:, :, c * w:(c + 1) * w])
+            nc.sync.dma_start(out=ks[:].rearrange("p (tt f) -> p tt f", tt=2), in_=k_v[:, :, c * w:(c + 1) * w])
+            nc.sync.dma_start(
+                out=cks[:].rearrange("p (n f) -> p n f", f=256),
+                in_=ck_v[:, c * CB * H:(c + 1) * CB * H, :],
+            )
+            nc.sync.dma_start(
+                out=vst[:].rearrange("p n j d -> p n (j d)")[:, :, 0:256],
+                in_=cv_v[:, c * CB * H:(c + 1) * CB * H, :],
+            )
+            chunks[c] = (xs, qs, ks, cks, vst)
+
+        w_sb = const.tile([P, 4 * E], BF16, name="w_sb")
+        nc.sync.dma_start(out=w_sb[:].rearrange("p (ob k) -> p ob k", ob=4), in_=Wv.rearrange("(ob p) k -> p ob k", p=P))
+        load_chunk(0)
+        bias_bf = const.tile([P, E], BF16, name="bias_bf")
+        nc.sync.dma_start(out=bias_bf[:], in_=bv.partition_broadcast(P))
+        load_chunk(1)
+
+        ident_f = const.tile([P, P], F32, name="ident_f")
+        make_identity(nc, ident_f[:])
+        ident_b = const.tile([P, P], BF16, name="ident_b")
+        make_identity(nc, ident_b[:])
+        mask_f = const.tile([P, P], F32, name="mask_f")
+        nc.gpsimd.memset(mask_f[:], 0.0)
+        nc.gpsimd.affine_select(
+            out=mask_f[:], in_=mask_f[:], compare_op=ALU.is_ge, fill=-1.0e10,
+            base=0, pattern=[[-1, P]], channel_multiplier=1,
+        )
+        mask_b = const.tile([P, P], BF16, name="mask_b")
+        nc.vector.tensor_copy(out=mask_b[:], in_=mask_f[:])
+        gts = []
+        for i in range(NG):
+            gt = const.tile([P, 2, P, 4], BF16, name="gt%d" % i, align_bytes=64)
+            nc.vector.memset(gt[:], 0.0)
+            gts.append(gt)
+        bias_f = const.tile([P, E], F32, name="bias_f")
+        nc.vector.tensor_copy(out=bias_f[:], in_=bias_bf[:])
+
+        if MANUAL:
+            ctx.enter_context(tc.manual_schedule())
+
+        w_w = w_sb[:].bitcast(F32)
+        w_g = const.tile([P, 4 * E], BF16, name="w_g", align_bytes=64)
+        w_gw = w_g[:].bitcast(F32).rearrange("p (ob o u) -> p ob o u", ob=4, u=2)
+        for half in range(2):
+            wt = ps_m.tile([P, 2, 2, P], F32, name="wt", tag="m")
+            for o2 in range(2):
+                for u in range(2):
+                    col = (half * 2 + o2) * 256 + u * P
+                    nc.tensor.transpose(wt[:, o2, u, :], w_w[:, col:col + P], ident_f[:])
+            nc.vector.tensor_copy(out=w_gw[:, half * 2:half * 2 + 2], in_=wt[:].rearrange("p ob u o -> p ob o u"))
+        wc = const.tile([P, E], U32, name="wc", align_bytes=64)
+        wsc = const.tile([P, E], U8, name="wsc", align_bytes=64)
+        nc.vector.quantize_mx(out=wc[:].bitcast(FP8X4), scales=wsc[:], in_=w_g[:])
+
+        def prep_x(b):
+            c, bb = divmod(b, CB)
+            xw = chunks[c][0][:].bitcast(F32)
+            xt = ps_m.tile([P, 2, 2, P], F32, name="xt", tag="m")
+            for tt in range(2):
+                for u in range(2):
+                    col = tt * (CB * 256) + bb * 256 + u * P
+                    nc.tensor.transpose(xt[:, tt, u, :], xw[:, col:col + P], ident_f[:])
+            xg = w2.tile([P, 1024], BF16, name="xg", tag="xg", align_bytes=64)
+            nc.vector.tensor_copy(
+                out=xg[:].bitcast(F32).rearrange("p (tt r u) -> p tt r u", tt=2, u=2),
+                in_=xt[:].rearrange("p tt u r -> p tt r u"),
+            )
+            st[("xg", b)] = xg
+
+        def quant_x(b):
+            xc = w2.tile([P, 256], U32, name="xc", tag="xc", align_bytes=64)
+            xsc = w2.tile([P, 256], U8, name="xsc", tag="xsc", align_bytes=64)
+            nc.vector.quantize_mx(out=xc[:].bitcast(FP8X4), scales=xsc[:], in_=st[("xg", b)][:])
+            st[("xc", b)] = (xc, xsc)
+            st[("vh", b)] = w2.tile([P, 2, E], F32, name="vh", tag="vh")
+
+        def proj(b, tt):
+            xc, xsc = st[("xc", b)]
+            vh = st[("vh", b)]
+            pp = ps_m.tile([P, E], F32, name="pp", tag="m")
+            nc.tensor.matmul_mx(
+                out=pp[:],
+                lhsT=xc[:, tt * P:(tt + 1) * P].bitcast(FP8X4), lhsT_scale=xsc[:, tt * P:(tt + 1) * P],
+                rhs=wc[:].bitcast(FP8X4), rhs_scale=wsc[:],
+                start=True, stop=True,
+            )
+            nc.vector.tensor_tensor(out=vh[:, tt, :], in0=pp[:], in1=bias_f[:], op=ALU.add)
+            nc.sync.dma_start(out=o1_v[:, b, tt], in_=vh[:, tt, :].rearrange("p (h d) -> p h d", h=H))
+
+        def cast_v(b):
+            c, bb = divmod(b, CB)
+            vst = chunks[c][4]
+            nc.gpsimd.tensor_scalar(
+                out=vst[:, bb * H:(bb + 1) * H, 2:4, :],
+                in0=st[("vh", b)][:].rearrange("p tt (h d) -> p h tt d", h=H),
+                scalar1=1.0, scalar2=0.0, op0=ALU.mult, op1=ALU.add,
+            )
+
+        def regroup_v(b):
+            c, bb = divmod(b, CB)
+            vst = chunks[c][4]
+            gv = w2.tile([P, H * D * 4], BF16, name="gv", tag="gv", align_bytes=64)
+            nc.vector.tensor_copy(
+                out=gv[:].rearrange("p (h d j) -> p h d j", h=H, j=4),
+                in_=vst[:, bb * H:(bb + 1) * H, :, :].rearrange("p h j d -> p h d j"),
+            )
+            st[("gv", b)] = gv
+
+        def quant_v(b):
+            vc = w3.tile([P, H * D], U32, name="vc", tag="vc", align_bytes=64)
+            vsc = w3.tile([P, H * D], U8, name="vsc", tag="vsc", align_bytes=64)
+            nc.vector.quantize_mx(out=vc[:].bitcast(FP8X4), scales=vsc[:], in_=st[("gv", b)][:])
+            st[("vc", b)] = (vc, vsc)
+
+        def prep_q(b):
+            c, bb = divmod(b, CB)
+            qs = chunks[c][1]
+            tp = ps_m.tile([P, 8, P], BF16, name="tq", tag="m")
+            for h in range(H):
+                for tt in range(2):
+                    col = tt * (CB * E) + bb * E + h * D
+                    nc.tensor.transpose(tp[:, h * 2 + tt, :], qs[:, col:col + D], ident_b[:])
+            qT = w2.tile([P, 8 * P], BF16, name="qT", tag="qT")
+            nc.scalar.copy(out=qT[:], in_=tp[:].rearrange("p a m -> p (a m)"))
+            st[("qT", b)] = qT
+
+        def prep_k(b, hp):
+            c, bb = divmod(b, CB)
+            ks, cks = chunks[c][2], chunks[c][3]
+            tp = ps_m.tile([P, 8, P], BF16, name="tk", tag="m")
+            for h2 in range(2):
+                h = hp * 2 + h2
+                for j in range(2):
+                    col = (bb * H + h) * 256 + j * D
+                    nc.tensor.transpose(tp[:, h2 * 4 + j, :], cks[:, col:col + D], ident_b[:])
+                for tt in range(2):
+                    col = tt * (CB * E) + bb * E + h * D
+                    nc.tensor.transpose(tp[:, h2 * 4 + 2 + tt, :], ks[:, col:col + D], ident_b[:])
+            kT = w4.tile([P, 8 * P], BF16, name="kT", tag="kT")
+            nc.scalar.copy(out=kT[:], in_=tp[:].rearrange("p a m -> p (a m)"))
+            st[("kT", b, hp)] = kT
+
+        def scores(g):
+            b, h = divmod(g, H)
+            qT = st[("qT", b)]
+            kT = st[("kT", b, h // 2)]
+            k0 = (h % 2) * 512
+            nmax = w4.tile([P, 2], F32, name="nmax", tag="nmax")
+            rsum = w4.tile([P, 2], F32, name="rsum", tag="rsum")
+            e = w3.tile([P, 896], BF16, name="e", tag="e")
+            for qt in range(2):
+                wd = 256 + qt * P
+                wa = wd + P
+                lq = qT[:, (h * 2 + qt) * P:(h * 2 + qt + 1) * P]
+                s = ps_s.tile([P, 512], F32, name="s", tag="s")
+                nc.tensor.matmul(s[:, 0:wd], lhsT=lq, rhs=kT[:, k0:k0 + wd], start=True, stop=True)
+                nc.tensor.matmul(s[:, wd:wa], lhsT=ident_b[:], rhs=mask_b[:], start=True, stop=False)
+                nc.tensor.matmul(s[:, wd:wa], lhsT=lq, rhs=kT[:, k0 + wd:k0 + wa], start=False, stop=True)
+                nc.vector.tensor_reduce(out=nmax[:, qt:qt + 1], in_=s[:, 0:wa], axis=AX.X, op=ALU.max, negate=True)
+                nc.scalar.activation(
+                    out=e[:, qt * 384:qt * 384 + wa], in_=s[:, 0:wa], func=ACT.Exp,
+                    bias=nmax[:, qt:qt + 1], scale=1.0, accum_out=rsum[:, qt:qt + 1],
+                )
+            st[("e", g)] = e
+            st[("rsum", g)] = rsum
+
+        def e_transpose(g):
+            e = st[("e", g)]
+            gt = gts[g % NG]
+            for qt in range(2):
+                nj = 3 + qt
+                et = ps_e.tile([P, 4, P], BF16, name="et", tag="et")
+                for j in range(nj):
+                    col = qt * 384 + j * P
+                    nc.tensor.transpose(et[:, j, :], e[:, col:col + P], ident_b[:])
+                nc.scalar.copy(out=gt[:, qt, :, 0:nj], in_=et[:, 0:nj, :].rearrange("p j m -> p m j"))
+
+        def quant_e(g):
+            gt = gts[g % NG]
+            ec = w3.tile([P, 256], U32, name="ec", tag="ec", align_bytes=64)
+            esc = w3.tile([P, 256], U8, name="esc", tag="esc", align_bytes=64)
+            nc.vector.quantize_mx(out=ec[:].bitcast(FP8X4), scales=esc[:], in_=gt[:].rearrange("p a m j -> p (a m j)"))
+            st[("ec", g)] = (ec, esc)
+
+        def pv(g):
+            b, h = divmod(g, H)
+            ec, esc = st[("ec", g)]
+            vc, vsc = st[("vc", b)]
+            if h == 0:
+                st[("ob", b)] = w3.tile([P, 2, E], F32, name="ob", tag="ob")
+            ob = st[("ob", b)]
+            o = ps_m.tile([P, 2, P], F32, name="o", tag="m")
+            for qt in range(2):
+                nc.tensor.matmul_mx(
+                    out=o[:, qt, :],
+                    lhsT=ec[:, qt * P:(qt + 1) * P].bitcast(FP8X4), lhsT_scale=esc[:, qt * P:(qt + 1) * P],
+                    rhs=vc[:, h * D:(h + 1) * D].bitcast(FP8X4), rhs_scale=vsc[:, h * D:(h + 1) * D],
+                    start=True, stop=True,
+                )
+            rinv = w3.tile([P, 2], F32, name="rinv", tag="rinv")
+            nc.vector.reciprocal(out=rinv[:], in_=st[("rsum", g)][:])
+            nc.vector.tensor_tensor(
+                out=ob[:, :, h * D:(h + 1) * D], in0=o[:],
+                in1=rinv[:].unsqueeze(2).to_broadcast([P, 2, D]), op=ALU.mult,
+            )
+            if h == H - 1:
+                nc.sync.dma_start(out=o0_v[:, :, b, :], in_=ob[:])
+
+        prep_x(0)
+        prep_q(0)
+        quant_x(0)
+        prep_k(0, 0)
+        proj(0, 0)
+        proj(0, 1)
+        prep_k(0, 1)
+        cast_v(0)
+        regroup_v(0)
+
+        for k in range(NH + 2):
+            b, r = divmod(k, H)
+            nb = b + 1
+            if r == 0 and b % CB == 0 and b // CB + 2 < NCH:
+                load_chunk(b // CB + 2)
+            if k < NH:
+                scores(k)
+            if r == 0 and b < B:
+                quant_v(b)
+            if 0 <= k - 2 < NH:
+                quant_e(k - 2)
+            if nb < B:
+                if r == 0:
+                    prep_x(nb)
+                elif r == 1:
+                    prep_q(nb)
+                elif r == 2:
+                    prep_k(nb, 0)
+                else:
+                    prep_k(nb, 1)
+            if 0 <= k - 1 < NH:
+                e_transpose(k - 1)
+            if 0 <= k - 2 < NH:
+                pv(k - 2)
+            if nb < B:
+                if r == 0:
+                    quant_x(nb)
+                elif r == 1:
+                    proj(nb, 0)
+                elif r == 2:
+                    proj(nb, 1)
+                    cast_v(nb)
+                else:
+                    regroup_v(nb)

@@ -18,10 +18,15 @@ P = 128
 NH = B * H
 FLOPS = 2 * T * B * E * E + 2 * 2 * NH * T * (C + T) * D
 
-MANUAL = False
 NG = 3
 CB = 2
 NCH = B // CB
+FIRST = -7
+
+PREP = {
+    "Tx": -7, "Cx": -6, "qx": -5, "pj0": -4, "pj1": -3, "cast": -3, "rgA": -2, "rgB": -1, "qv": 0,
+    "Tq": -5, "Cq": -4, "Tk0": -4, "Ck0": -3, "Tk1": -2, "Ck1": -1,
+}
 
 
 def tile_multiheadlmattentionwithcache_pa_t_kernel(
@@ -34,6 +39,7 @@ def tile_multiheadlmattentionwithcache_pa_t_kernel(
         w2 = ctx.enter_context(tc.tile_pool(name="w2", bufs=2))
         w3 = ctx.enter_context(tc.tile_pool(name="w3", bufs=3))
         w4 = ctx.enter_context(tc.tile_pool(name="w4", bufs=4))
+        w6 = ctx.enter_context(tc.tile_pool(name="w6", bufs=6))
         ps_s = ctx.enter_context(tc.psum_pool(name="ps_s", bufs=3))
         ps_e = ctx.enter_context(tc.psum_pool(name="ps_e", bufs=2))
         ps_m = ctx.enter_context(tc.psum_pool(name="ps_m", bufs=3))
@@ -69,11 +75,14 @@ def tile_multiheadlmattentionwithcache_pa_t_kernel(
             )
             chunks[c] = (xs, qs, ks, cks, vst)
 
+        b_row = const.tile([P, E], BF16, name="b_row")
+        nc.vector.memset(b_row[:], 0.0)
+        nc.sync.dma_start(out=b_row[0:1, :], in_=bv.rearrange("(o e) -> o e", o=1))
+        ones_b = const.tile([P, P], BF16, name="ones_b")
+        nc.vector.memset(ones_b[:], 1.0)
         w_sb = const.tile([P, 4 * E], BF16, name="w_sb")
         nc.sync.dma_start(out=w_sb[:].rearrange("p (ob k) -> p ob k", ob=4), in_=Wv.rearrange("(ob p) k -> p ob k", p=P))
         load_chunk(0)
-        bias_bf = const.tile([P, E], BF16, name="bias_bf")
-        nc.sync.dma_start(out=bias_bf[:], in_=bv.partition_broadcast(P))
         load_chunk(1)
 
         ident_f = const.tile([P, P], F32, name="ident_f")
@@ -93,11 +102,8 @@ def tile_multiheadlmattentionwithcache_pa_t_kernel(
             gt = const.tile([P, 2, P, 4], BF16, name="gt%d" % i, align_bytes=64)
             nc.vector.memset(gt[:], 0.0)
             gts.append(gt)
-        bias_f = const.tile([P, E], F32, name="bias_f")
-        nc.vector.tensor_copy(out=bias_f[:], in_=bias_bf[:])
 
-        if MANUAL:
-            ctx.enter_context(tc.manual_schedule())
+        ctx.enter_context(tc.manual_schedule())
 
         w_w = w_sb[:].bitcast(F32)
         w_g = const.tile([P, 4 * E], BF16, name="w_g", align_bytes=64)
@@ -112,8 +118,12 @@ def tile_multiheadlmattentionwithcache_pa_t_kernel(
         wc = const.tile([P, E], U32, name="wc", align_bytes=64)
         wsc = const.tile([P, E], U8, name="wsc", align_bytes=64)
         nc.vector.quantize_mx(out=wc[:].bitcast(FP8X4), scales=wsc[:], in_=w_g[:])
+        bias_ps = ps_m.tile([P, E], F32, name="bias_ps", tag="m")
+        nc.tensor.matmul(bias_ps[:], lhsT=ones_b[:], rhs=b_row[:], start=True, stop=True)
+        bias_f = const.tile([P, E], F32, name="bias_f")
+        nc.vector.tensor_copy(out=bias_f[:], in_=bias_ps[:])
 
-        def prep_x(b):
+        def t_x(b):
             c, bb = divmod(b, CB)
             xw = chunks[c][0][:].bitcast(F32)
             xt = ps_m.tile([P, 2, 2, P], F32, name="xt", tag="m")
@@ -121,10 +131,13 @@ def tile_multiheadlmattentionwithcache_pa_t_kernel(
                 for u in range(2):
                     col = tt * (CB * 256) + bb * 256 + u * P
                     nc.tensor.transpose(xt[:, tt, u, :], xw[:, col:col + P], ident_f[:])
+            st[("xt", b)] = xt
+
+        def c_x(b):
             xg = w2.tile([P, 1024], BF16, name="xg", tag="xg", align_bytes=64)
             nc.vector.tensor_copy(
                 out=xg[:].bitcast(F32).rearrange("p (tt r u) -> p tt r u", tt=2, u=2),
-                in_=xt[:].rearrange("p tt u r -> p tt r u"),
+                in_=st[("xt", b)][:].rearrange("p tt u r -> p tt r u"),
             )
             st[("xg", b)] = xg
 
@@ -135,9 +148,8 @@ def tile_multiheadlmattentionwithcache_pa_t_kernel(
             st[("xc", b)] = (xc, xsc)
             st[("vh", b)] = w2.tile([P, 2, E], F32, name="vh", tag="vh")
 
-        def proj(b, tt):
+        def pj_mm(b, tt):
             xc, xsc = st[("xc", b)]
-            vh = st[("vh", b)]
             pp = ps_m.tile([P, E], F32, name="pp", tag="m")
             nc.tensor.matmul_mx(
                 out=pp[:],
@@ -145,7 +157,11 @@ def tile_multiheadlmattentionwithcache_pa_t_kernel(
                 rhs=wc[:].bitcast(FP8X4), rhs_scale=wsc[:],
                 start=True, stop=True,
             )
-            nc.vector.tensor_tensor(out=vh[:, tt, :], in0=pp[:], in1=bias_f[:], op=ALU.add)
+            st[("pp", b, tt)] = pp
+
+        def pj_add(b, tt):
+            vh = st[("vh", b)]
+            nc.vector.tensor_tensor(out=vh[:, tt, :], in0=st[("pp", b, tt)][:], in1=bias_f[:], op=ALU.add)
             nc.sync.dma_start(out=o1_v[:, b, tt], in_=vh[:, tt, :].rearrange("p (h d) -> p h d", h=H))
 
         def cast_v(b):
@@ -157,15 +173,18 @@ def tile_multiheadlmattentionwithcache_pa_t_kernel(
                 scalar1=1.0, scalar2=0.0, op0=ALU.mult, op1=ALU.add,
             )
 
-        def regroup_v(b):
+        def regroup_v(b, half):
             c, bb = divmod(b, CB)
             vst = chunks[c][4]
-            gv = w2.tile([P, H * D * 4], BF16, name="gv", tag="gv", align_bytes=64)
-            nc.vector.tensor_copy(
-                out=gv[:].rearrange("p (h d j) -> p h d j", h=H, j=4),
-                in_=vst[:, bb * H:(bb + 1) * H, :, :].rearrange("p h j d -> p h d j"),
-            )
-            st[("gv", b)] = gv
+            if half == 0:
+                st[("gv", b)] = w2.tile([P, H * D * 4], BF16, name="gv", tag="gv", align_bytes=64)
+            gv = st[("gv", b)]
+            for h2 in range(2):
+                h = half * 2 + h2
+                nc.vector.tensor_copy(
+                    out=gv[:, h * 512:(h + 1) * 512].rearrange("p (c i j) -> p c j i", i=4, j=4),
+                    in_=vst[:, bb * H + h, :, :].rearrange("p j (c i) -> p c j i", i=4),
+                )
 
         def quant_v(b):
             vc = w3.tile([P, H * D], U32, name="vc", tag="vc", align_bytes=64)
@@ -173,7 +192,7 @@ def tile_multiheadlmattentionwithcache_pa_t_kernel(
             nc.vector.quantize_mx(out=vc[:].bitcast(FP8X4), scales=vsc[:], in_=st[("gv", b)][:])
             st[("vc", b)] = (vc, vsc)
 
-        def prep_q(b):
+        def t_q(b):
             c, bb = divmod(b, CB)
             qs = chunks[c][1]
             tp = ps_m.tile([P, 8, P], BF16, name="tq", tag="m")
@@ -181,11 +200,14 @@ def tile_multiheadlmattentionwithcache_pa_t_kernel(
                 for tt in range(2):
                     col = tt * (CB * E) + bb * E + h * D
                     nc.tensor.transpose(tp[:, h * 2 + tt, :], qs[:, col:col + D], ident_b[:])
+            st[("tq", b)] = tp
+
+        def c_q(b):
             qT = w2.tile([P, 8 * P], BF16, name="qT", tag="qT")
-            nc.scalar.copy(out=qT[:], in_=tp[:].rearrange("p a m -> p (a m)"))
+            nc.scalar.copy(out=qT[:], in_=st[("tq", b)][:].rearrange("p a m -> p (a m)"))
             st[("qT", b)] = qT
 
-        def prep_k(b, hp):
+        def t_k(b, hp):
             c, bb = divmod(b, CB)
             ks, cks = chunks[c][2], chunks[c][3]
             tp = ps_m.tile([P, 8, P], BF16, name="tk", tag="m")
@@ -197,59 +219,70 @@ def tile_multiheadlmattentionwithcache_pa_t_kernel(
                 for tt in range(2):
                     col = tt * (CB * E) + bb * E + h * D
                     nc.tensor.transpose(tp[:, h2 * 4 + 2 + tt, :], ks[:, col:col + D], ident_b[:])
+            st[("tk", b, hp)] = tp
+
+        def c_k(b, hp):
             kT = w4.tile([P, 8 * P], BF16, name="kT", tag="kT")
-            nc.scalar.copy(out=kT[:], in_=tp[:].rearrange("p a m -> p (a m)"))
+            nc.scalar.copy(out=kT[:], in_=st[("tk", b, hp)][:].rearrange("p a m -> p (a m)"))
             st[("kT", b, hp)] = kT
 
-        def scores(g):
+        def sc_mm(g, qt):
             b, h = divmod(g, H)
             qT = st[("qT", b)]
             kT = st[("kT", b, h // 2)]
             k0 = (h % 2) * 512
-            nmax = w4.tile([P, 2], F32, name="nmax", tag="nmax")
-            rsum = w4.tile([P, 2], F32, name="rsum", tag="rsum")
-            e = w3.tile([P, 896], BF16, name="e", tag="e")
-            for qt in range(2):
-                wd = 256 + qt * P
-                wa = wd + P
-                lq = qT[:, (h * 2 + qt) * P:(h * 2 + qt + 1) * P]
-                s = ps_s.tile([P, 512], F32, name="s", tag="s")
-                nc.tensor.matmul(s[:, 0:wd], lhsT=lq, rhs=kT[:, k0:k0 + wd], start=True, stop=True)
-                nc.tensor.matmul(s[:, wd:wa], lhsT=ident_b[:], rhs=mask_b[:], start=True, stop=False)
-                nc.tensor.matmul(s[:, wd:wa], lhsT=lq, rhs=kT[:, k0 + wd:k0 + wa], start=False, stop=True)
-                nc.vector.tensor_reduce(out=nmax[:, qt:qt + 1], in_=s[:, 0:wa], axis=AX.X, op=ALU.max, negate=True)
-                nc.scalar.activation(
-                    out=e[:, qt * 384:qt * 384 + wa], in_=s[:, 0:wa], func=ACT.Exp,
-                    bias=nmax[:, qt:qt + 1], scale=1.0, accum_out=rsum[:, qt:qt + 1],
-                )
-            st[("e", g)] = e
-            st[("rsum", g)] = rsum
+            if qt == 0:
+                st[("nmax", g)] = w3.tile([P, 2], F32, name="nmax", tag="nmax")
+                st[("rsum", g)] = w6.tile([P, 2], F32, name="rsum", tag="rsum")
+                st[("e", g)] = w3.tile([P, 896], BF16, name="e", tag="e")
+            wd = 256 + qt * P
+            wa = wd + P
+            lq = qT[:, (h * 2 + qt) * P:(h * 2 + qt + 1) * P]
+            s = ps_s.tile([P, 512], F32, name="s", tag="s")
+            nc.tensor.matmul(s[:, 0:wd], lhsT=lq, rhs=kT[:, k0:k0 + wd], start=True, stop=True)
+            nc.tensor.matmul(s[:, wd:wa], lhsT=ident_b[:], rhs=mask_b[:], start=True, stop=False)
+            nc.tensor.matmul(s[:, wd:wa], lhsT=lq, rhs=kT[:, k0 + wd:k0 + wa], start=False, stop=True)
+            st[("s", g, qt)] = s
 
-        def e_transpose(g):
+        def sc_max(g, qt):
+            wa = 384 + qt * P
+            nc.vector.tensor_reduce(
+                out=st[("nmax", g)][:, qt:qt + 1], in_=st[("s", g, qt)][:, 0:wa], axis=AX.X, op=ALU.max, negate=True
+            )
+
+        def sc_exp(g, qt):
+            wa = 384 + qt * P
+            nc.scalar.activation(
+                out=st[("e", g)][:, qt * 384:qt * 384 + wa], in_=st[("s", g, qt)][:, 0:wa], func=ACT.Exp,
+                bias=st[("nmax", g)][:, qt:qt + 1], scale=1.0, accum_out=st[("rsum", g)][:, qt:qt + 1],
+            )
+
+        def et_t(g, qt):
             e = st[("e", g)]
-            gt = gts[g % NG]
-            for qt in range(2):
-                nj = 3 + qt
-                et = ps_e.tile([P, 4, P], BF16, name="et", tag="et")
-                for j in range(nj):
-                    col = qt * 384 + j * P
-                    nc.tensor.transpose(et[:, j, :], e[:, col:col + P], ident_b[:])
-                nc.scalar.copy(out=gt[:, qt, :, 0:nj], in_=et[:, 0:nj, :].rearrange("p j m -> p m j"))
+            et = ps_e.tile([P, 4, P], BF16, name="et", tag="et")
+            for j in range(3 + qt):
+                col = qt * 384 + j * P
+                nc.tensor.transpose(et[:, j, :], e[:, col:col + P], ident_b[:])
+            st[("et", g, qt)] = et
+
+        def et_evac(g, qt):
+            nj = 3 + qt
+            nc.scalar.copy(
+                out=gts[g % NG][:, qt, :, 0:nj], in_=st[("et", g, qt)][:, 0:nj, :].rearrange("p j m -> p m j")
+            )
 
         def quant_e(g):
-            gt = gts[g % NG]
             ec = w3.tile([P, 256], U32, name="ec", tag="ec", align_bytes=64)
             esc = w3.tile([P, 256], U8, name="esc", tag="esc", align_bytes=64)
-            nc.vector.quantize_mx(out=ec[:].bitcast(FP8X4), scales=esc[:], in_=gt[:].rearrange("p a m j -> p (a m j)"))
+            nc.vector.quantize_mx(
+                out=ec[:].bitcast(FP8X4), scales=esc[:], in_=gts[g % NG][:].rearrange("p a m j -> p (a m j)")
+            )
             st[("ec", g)] = (ec, esc)
 
-        def pv(g):
+        def pv_mm(g):
             b, h = divmod(g, H)
             ec, esc = st[("ec", g)]
             vc, vsc = st[("vc", b)]
-            if h == 0:
-                st[("ob", b)] = w3.tile([P, 2, E], F32, name="ob", tag="ob")
-            ob = st[("ob", b)]
             o = ps_m.tile([P, 2, P], F32, name="o", tag="m")
             for qt in range(2):
                 nc.tensor.matmul_mx(
@@ -258,56 +291,94 @@ def tile_multiheadlmattentionwithcache_pa_t_kernel(
                     rhs=vc[:, h * D:(h + 1) * D].bitcast(FP8X4), rhs_scale=vsc[:, h * D:(h + 1) * D],
                     start=True, stop=True,
                 )
+            st[("o", g)] = o
+
+        def pv_out(g):
+            b, h = divmod(g, H)
+            if h == 0:
+                st[("ob", b)] = w3.tile([P, 2, E], F32, name="ob", tag="ob")
+            ob = st[("ob", b)]
             rinv = w3.tile([P, 2], F32, name="rinv", tag="rinv")
             nc.vector.reciprocal(out=rinv[:], in_=st[("rsum", g)][:])
             nc.vector.tensor_tensor(
-                out=ob[:, :, h * D:(h + 1) * D], in0=o[:],
+                out=ob[:, :, h * D:(h + 1) * D], in0=st[("o", g)][:],
                 in1=rinv[:].unsqueeze(2).to_broadcast([P, 2, D]), op=ALU.mult,
             )
             if h == H - 1:
                 nc.sync.dma_start(out=o0_v[:, :, b, :], in_=ob[:])
 
-        prep_x(0)
-        prep_q(0)
-        quant_x(0)
-        prep_k(0, 0)
-        proj(0, 0)
-        proj(0, 1)
-        prep_k(0, 1)
-        cast_v(0)
-        regroup_v(0)
+        def batch_at(k, step):
+            nb, rem = divmod(k - PREP[step], H)
+            if rem == 0 and 0 <= nb < B:
+                return nb
+            return -1
 
-        for k in range(NH + 2):
-            b, r = divmod(k, H)
-            nb = b + 1
-            if r == 0 and b % CB == 0 and b // CB + 2 < NCH:
-                load_chunk(b // CB + 2)
-            if k < NH:
-                scores(k)
-            if r == 0 and b < B:
-                quant_v(b)
-            if 0 <= k - 2 < NH:
+        def head_ok(g):
+            return 0 <= g < NH
+
+        for k in range(FIRST, NH + 4):
+            if k >= 0 and k % (CB * H) == 0 and k // (CB * H) + 2 < NCH:
+                load_chunk(k // (CB * H) + 2)
+            if head_ok(k):
+                sc_max(k, 0)
+                sc_exp(k, 0)
+                sc_max(k, 1)
+                sc_exp(k, 1)
+            if head_ok(k - 2):
                 quant_e(k - 2)
-            if nb < B:
-                if r == 0:
-                    prep_x(nb)
-                elif r == 1:
-                    prep_q(nb)
-                elif r == 2:
-                    prep_k(nb, 0)
-                else:
-                    prep_k(nb, 1)
-            if 0 <= k - 1 < NH:
-                e_transpose(k - 1)
-            if 0 <= k - 2 < NH:
-                pv(k - 2)
-            if nb < B:
-                if r == 0:
-                    quant_x(nb)
-                elif r == 1:
-                    proj(nb, 0)
-                elif r == 2:
-                    proj(nb, 1)
-                    cast_v(nb)
-                else:
-                    regroup_v(nb)
+            if head_ok(k - 3):
+                pv_mm(k - 3)
+            for tt in range(2):
+                nb = batch_at(k, "pj%d" % tt)
+                if nb >= 0:
+                    pj_mm(nb, tt)
+            if head_ok(k - 3):
+                pv_out(k - 3)
+            nb = batch_at(k, "Cq")
+            if nb >= 0:
+                c_q(nb)
+            for hp in range(2):
+                nb = batch_at(k, "Ck%d" % hp)
+                if nb >= 0:
+                    c_k(nb, hp)
+            if head_ok(k + 1):
+                sc_mm(k + 1, 0)
+            if head_ok(k - 1):
+                et_t(k - 1, 0)
+                et_evac(k - 1, 0)
+                et_t(k - 1, 1)
+                et_evac(k - 1, 1)
+            if head_ok(k + 1):
+                sc_mm(k + 1, 1)
+            nb = batch_at(k, "Tx")
+            if nb >= 0:
+                t_x(nb)
+            nb = batch_at(k, "Tq")
+            if nb >= 0:
+                t_q(nb)
+            for hp in range(2):
+                nb = batch_at(k, "Tk%d" % hp)
+                if nb >= 0:
+                    t_k(nb, hp)
+            nb = batch_at(k, "Cx")
+            if nb >= 0:
+                c_x(nb)
+            nb = batch_at(k, "qx")
+            if nb >= 0:
+                quant_x(nb)
+            for tt in range(2):
+                nb = batch_at(k, "pj%d" % tt)
+                if nb >= 0:
+                    pj_add(nb, tt)
+            nb = batch_at(k, "cast")
+            if nb >= 0:
+                cast_v(nb)
+            nb = batch_at(k, "rgA")
+            if nb >= 0:
+                regroup_v(nb, 0)
+            nb = batch_at(k, "rgB")
+            if nb >= 0:
+                regroup_v(nb, 1)
+            nb = batch_at(k, "qv")
+            if nb >= 0:
+                quant_v(nb)

@@ -18,15 +18,10 @@ P = 128
 NH = B * H
 FLOPS = 2 * T * B * E * E + 2 * 2 * NH * T * (C + T) * D
 
-NG = 3
+NG = 4
 CB = 2
 NCH = B // CB
 FIRST = -7
-
-PREP = {
-    "Tx": -7, "Cx": -6, "qx": -5, "pj0": -4, "pj1": -3, "cast": -3, "rgA": -2, "rgB": -1, "qv": 0,
-    "Tq": -5, "Cq": -4, "Tk0": -4, "Ck0": -3, "Tk1": -2, "Ck1": -1,
-}
 
 
 def tile_multiheadlmattentionwithcache_pa_t_kernel(
@@ -39,7 +34,7 @@ def tile_multiheadlmattentionwithcache_pa_t_kernel(
         w2 = ctx.enter_context(tc.tile_pool(name="w2", bufs=2))
         w3 = ctx.enter_context(tc.tile_pool(name="w3", bufs=3))
         w4 = ctx.enter_context(tc.tile_pool(name="w4", bufs=4))
-        w6 = ctx.enter_context(tc.tile_pool(name="w6", bufs=6))
+        w5 = ctx.enter_context(tc.tile_pool(name="w5", bufs=5))
         ps_s = ctx.enter_context(tc.psum_pool(name="ps_s", bufs=3))
         ps_e = ctx.enter_context(tc.psum_pool(name="ps_e", bufs=2))
         ps_m = ctx.enter_context(tc.psum_pool(name="ps_m", bufs=3))
@@ -233,8 +228,9 @@ def tile_multiheadlmattentionwithcache_pa_t_kernel(
             k0 = (h % 2) * 512
             if qt == 0:
                 st[("nmax", g)] = w3.tile([P, 2], F32, name="nmax", tag="nmax")
-                st[("rsum", g)] = w6.tile([P, 2], F32, name="rsum", tag="rsum")
-                st[("e", g)] = w3.tile([P, 896], BF16, name="e", tag="e")
+                st[("e", g)] = w4.tile([P, 896], BF16, name="e", tag="e")
+                if g % 2 == 0:
+                    st[("rsum", g // 2)] = w5.tile([P, 4], F32, name="rsum", tag="rsum")
             wd = 256 + qt * P
             wa = wd + P
             lq = qT[:, (h * 2 + qt) * P:(h * 2 + qt + 1) * P]
@@ -254,7 +250,8 @@ def tile_multiheadlmattentionwithcache_pa_t_kernel(
             wa = 384 + qt * P
             nc.scalar.activation(
                 out=st[("e", g)][:, qt * 384:qt * 384 + wa], in_=st[("s", g, qt)][:, 0:wa], func=ACT.Exp,
-                bias=st[("nmax", g)][:, qt:qt + 1], scale=1.0, accum_out=st[("rsum", g)][:, qt:qt + 1],
+                bias=st[("nmax", g)][:, qt:qt + 1], scale=1.0,
+                accum_out=st[("rsum", g // 2)][:, (g % 2) * 2 + qt:(g % 2) * 2 + qt + 1],
             )
 
         def et_t(g, qt):
@@ -298,87 +295,69 @@ def tile_multiheadlmattentionwithcache_pa_t_kernel(
             if h == 0:
                 st[("ob", b)] = w3.tile([P, 2, E], F32, name="ob", tag="ob")
             ob = st[("ob", b)]
-            rinv = w3.tile([P, 2], F32, name="rinv", tag="rinv")
-            nc.vector.reciprocal(out=rinv[:], in_=st[("rsum", g)][:])
+            if g % 2 == 0:
+                st[("rinv", g // 2)] = w3.tile([P, 4], F32, name="rinv", tag="rinv")
+                nc.vector.reciprocal(out=st[("rinv", g // 2)][:], in_=st[("rsum", g // 2)][:])
+            rinv = st[("rinv", g // 2)][:, (g % 2) * 2:(g % 2) * 2 + 2]
             nc.vector.tensor_tensor(
                 out=ob[:, :, h * D:(h + 1) * D], in0=st[("o", g)][:],
-                in1=rinv[:].unsqueeze(2).to_broadcast([P, 2, D]), op=ALU.mult,
+                in1=rinv.unsqueeze(2).to_broadcast([P, 2, D]), op=ALU.mult,
             )
             if h == H - 1:
                 nc.sync.dma_start(out=o0_v[:, :, b, :], in_=ob[:])
 
-        def batch_at(k, step):
-            nb, rem = divmod(k - PREP[step], H)
-            if rem == 0 and 0 <= nb < B:
-                return nb
-            return -1
+        def on(batch, step, *args):
+            if 0 <= batch < B:
+                step(batch, *args)
 
-        def head_ok(g):
-            return 0 <= g < NH
+        def head(g, step, *args):
+            if 0 <= g < NH:
+                step(g, *args)
 
-        for k in range(FIRST, NH + 4):
+        for k in range(FIRST, NH + 5):
+            b, r = divmod(k, H)
             if k >= 0 and k % (CB * H) == 0 and k // (CB * H) + 2 < NCH:
                 load_chunk(k // (CB * H) + 2)
-            if head_ok(k):
-                sc_max(k, 0)
-                sc_exp(k, 0)
-                sc_max(k, 1)
-                sc_exp(k, 1)
-            if head_ok(k - 2):
-                quant_e(k - 2)
-            if head_ok(k - 3):
-                pv_mm(k - 3)
-            for tt in range(2):
-                nb = batch_at(k, "pj%d" % tt)
-                if nb >= 0:
-                    pj_mm(nb, tt)
-            if head_ok(k - 3):
-                pv_out(k - 3)
-            nb = batch_at(k, "Cq")
-            if nb >= 0:
-                c_q(nb)
-            for hp in range(2):
-                nb = batch_at(k, "Ck%d" % hp)
-                if nb >= 0:
-                    c_k(nb, hp)
-            if head_ok(k + 1):
-                sc_mm(k + 1, 0)
-            if head_ok(k - 1):
-                et_t(k - 1, 0)
-                et_evac(k - 1, 0)
-                et_t(k - 1, 1)
-                et_evac(k - 1, 1)
-            if head_ok(k + 1):
-                sc_mm(k + 1, 1)
-            nb = batch_at(k, "Tx")
-            if nb >= 0:
-                t_x(nb)
-            nb = batch_at(k, "Tq")
-            if nb >= 0:
-                t_q(nb)
-            for hp in range(2):
-                nb = batch_at(k, "Tk%d" % hp)
-                if nb >= 0:
-                    t_k(nb, hp)
-            nb = batch_at(k, "Cx")
-            if nb >= 0:
-                c_x(nb)
-            nb = batch_at(k, "qx")
-            if nb >= 0:
-                quant_x(nb)
-            for tt in range(2):
-                nb = batch_at(k, "pj%d" % tt)
-                if nb >= 0:
-                    pj_add(nb, tt)
-            nb = batch_at(k, "cast")
-            if nb >= 0:
-                cast_v(nb)
-            nb = batch_at(k, "rgA")
-            if nb >= 0:
-                regroup_v(nb, 0)
-            nb = batch_at(k, "rgB")
-            if nb >= 0:
-                regroup_v(nb, 1)
-            nb = batch_at(k, "qv")
-            if nb >= 0:
-                quant_v(nb)
+            if r == 0:
+                on(b + 1, c_q)
+            elif r == 1:
+                on(b + 1, c_k, 0)
+            elif r == 3:
+                on(b + 1, c_k, 1)
+            head(k, sc_max, 0)
+            head(k, sc_exp, 0)
+            head(k - 3, quant_e)
+            if r == 0:
+                on(b + 1, pj_mm, 0)
+            elif r == 1:
+                on(b + 1, pj_mm, 1)
+            head(k - 4, pv_mm)
+            head(k - 1, et_t, 0)
+            head(k - 1, et_evac, 0)
+            head(k + 1, sc_mm, 0)
+            head(k, sc_max, 1)
+            head(k, sc_exp, 1)
+            head(k - 1, et_t, 1)
+            head(k - 1, et_evac, 1)
+            head(k - 4, pv_out)
+            if r == 0:
+                on(b + 1, t_k, 0)
+            elif r == 1:
+                on(b + 2, t_x)
+            elif r == 2:
+                on(b + 1, t_k, 1)
+            else:
+                on(b + 2, t_q)
+            head(k + 1, sc_mm, 1)
+            if r == 0:
+                on(b + 1, pj_add, 0)
+                on(b, quant_v)
+            elif r == 1:
+                on(b + 1, pj_add, 1)
+                on(b + 1, cast_v)
+            elif r == 2:
+                on(b + 2, c_x)
+                on(b + 1, regroup_v, 0)
+            else:
+                on(b + 2, quant_x)
+                on(b + 1, regroup_v, 1)

@@ -50,25 +50,31 @@ def tile_multiheadlmattentionwithcache_pa_t_kernel(
         chunks = {}
         st = {}
 
-        def load_chunk(c):
+        def load_chunk(c, parts):
             w = CB * E
             xs = ld.tile([P, 2 * w], BF16, name="xs", tag="xs")
             qs = ld.tile([P, 2 * w], BF16, name="qs", tag="qs")
             ks = ld.tile([P, 2 * w], BF16, name="ks", tag="ks")
             cks = ld.tile([P, CB * H * 256], BF16, name="cks", tag="cks")
             vst = ld.tile([P, CB * H, 4, D], BF16, name="vst", tag="vst")
-            nc.sync.dma_start(out=xs[:].rearrange("p (tt f) -> p tt f", tt=2), in_=x_v[:, :, c * w:(c + 1) * w])
-            nc.sync.dma_start(out=qs[:].rearrange("p (tt f) -> p tt f", tt=2), in_=q_v[:, :, c * w:(c + 1) * w])
-            nc.sync.dma_start(out=ks[:].rearrange("p (tt f) -> p tt f", tt=2), in_=k_v[:, :, c * w:(c + 1) * w])
-            nc.sync.dma_start(
-                out=cks[:].rearrange("p (n f) -> p n f", f=256),
-                in_=ck_v[:, c * CB * H:(c + 1) * CB * H, :],
-            )
-            nc.sync.dma_start(
-                out=vst[:].rearrange("p n j d -> p n (j d)")[:, :, 0:256],
-                in_=cv_v[:, c * CB * H:(c + 1) * CB * H, :],
-            )
             chunks[c] = (xs, qs, ks, cks, vst)
+            wp = w // parts
+            nh = CB * H // parts
+            for i in range(parts):
+                for sb, dram in ((xs, x_v), (qs, q_v), (ks, k_v)):
+                    nc.sync.dma_start(
+                        out=sb[:].rearrange("p (tt f) -> p tt f", tt=2)[:, :, i * wp:(i + 1) * wp],
+                        in_=dram[:, :, c * w + i * wp:c * w + (i + 1) * wp],
+                    )
+                n0 = c * CB * H + i * nh
+                nc.sync.dma_start(
+                    out=cks[:].rearrange("p (n f) -> p n f", f=256)[:, i * nh:(i + 1) * nh, :],
+                    in_=ck_v[:, n0:n0 + nh, :],
+                )
+                nc.sync.dma_start(
+                    out=vst[:].rearrange("p n j d -> p n (j d)")[:, i * nh:(i + 1) * nh, 0:256],
+                    in_=cv_v[:, n0:n0 + nh, :],
+                )
 
         b_row = const.tile([P, E], BF16, name="b_row")
         nc.vector.memset(b_row[:], 0.0)
@@ -77,8 +83,8 @@ def tile_multiheadlmattentionwithcache_pa_t_kernel(
         nc.vector.memset(ones_b[:], 1.0)
         w_sb = const.tile([P, 4 * E], BF16, name="w_sb")
         nc.sync.dma_start(out=w_sb[:].rearrange("p (ob k) -> p ob k", ob=4), in_=Wv.rearrange("(ob p) k -> p ob k", p=P))
-        load_chunk(0)
-        load_chunk(1)
+        load_chunk(0, CB)
+        load_chunk(1, 1)
 
         ident_f = const.tile([P, P], F32, name="ident_f")
         make_identity(nc, ident_f[:])
@@ -130,7 +136,7 @@ def tile_multiheadlmattentionwithcache_pa_t_kernel(
 
         def c_x(b):
             xg = w2.tile([P, 1024], BF16, name="xg", tag="xg", align_bytes=64)
-            nc.vector.tensor_copy(
+            nc.scalar.copy(
                 out=xg[:].bitcast(F32).rearrange("p (tt r u) -> p tt r u", tt=2, u=2),
                 in_=st[("xt", b)][:].rearrange("p tt u r -> p tt r u"),
             )
@@ -303,7 +309,9 @@ def tile_multiheadlmattentionwithcache_pa_t_kernel(
                 out=ob[:, :, h * D:(h + 1) * D], in0=st[("o", g)][:],
                 in1=rinv.unsqueeze(2).to_broadcast([P, 2, D]), op=ALU.mult,
             )
-            if h == H - 1:
+            if b == B - 1:
+                nc.sync.dma_start(out=o0_v[:, :, b, h * D:(h + 1) * D], in_=ob[:, :, h * D:(h + 1) * D])
+            elif h == H - 1:
                 nc.sync.dma_start(out=o0_v[:, :, b, :], in_=ob[:])
 
         def on(batch, step, *args):
@@ -317,12 +325,14 @@ def tile_multiheadlmattentionwithcache_pa_t_kernel(
         for k in range(FIRST, NH + 5):
             b, r = divmod(k, H)
             if k >= 0 and k % (CB * H) == 0 and k // (CB * H) + 2 < NCH:
-                load_chunk(k // (CB * H) + 2)
+                load_chunk(k // (CB * H) + 2, 1)
             if r == 0:
                 on(b + 1, c_q)
             elif r == 1:
                 on(b + 1, c_k, 0)
-            elif r == 3:
+            elif r == 2:
+                on(b + 2, c_x)
+            else:
                 on(b + 1, c_k, 1)
             head(k, sc_max, 0)
             head(k, sc_exp, 0)
@@ -356,7 +366,6 @@ def tile_multiheadlmattentionwithcache_pa_t_kernel(
                 on(b + 1, pj_add, 1)
                 on(b + 1, cast_v)
             elif r == 2:
-                on(b + 2, c_x)
                 on(b + 1, regroup_v, 0)
             else:
                 on(b + 2, quant_x)

@@ -34,7 +34,6 @@ def tile_multiheadlmattentionwithcache_pa_t_kernel(
         w2 = ctx.enter_context(tc.tile_pool(name="w2", bufs=2))
         w3 = ctx.enter_context(tc.tile_pool(name="w3", bufs=3))
         w4 = ctx.enter_context(tc.tile_pool(name="w4", bufs=4))
-        w5 = ctx.enter_context(tc.tile_pool(name="w5", bufs=5))
         ps_s = ctx.enter_context(tc.psum_pool(name="ps_s", bufs=3))
         ps_e = ctx.enter_context(tc.psum_pool(name="ps_e", bufs=2))
         ps_m = ctx.enter_context(tc.psum_pool(name="ps_m", bufs=3))
@@ -165,12 +164,12 @@ def tile_multiheadlmattentionwithcache_pa_t_kernel(
             nc.vector.tensor_tensor(out=vh[:, tt, :], in0=st[("pp", b, tt)][:], in1=bias_f[:], op=ALU.add)
             nc.sync.dma_start(out=o1_v[:, b, tt], in_=vh[:, tt, :].rearrange("p (h d) -> p h d", h=H))
 
-        def cast_v(b):
+        def cast_v(b, tt):
             c, bb = divmod(b, CB)
             vst = chunks[c][4]
             nc.gpsimd.tensor_scalar(
-                out=vst[:, bb * H:(bb + 1) * H, 2:4, :],
-                in0=st[("vh", b)][:].rearrange("p tt (h d) -> p h tt d", h=H),
+                out=vst[:, bb * H:(bb + 1) * H, 2 + tt, :],
+                in0=st[("vh", b)][:, tt, :].rearrange("p (h d) -> p h d", h=H),
                 scalar1=1.0, scalar2=0.0, op0=ALU.mult, op1=ALU.add,
             )
 
@@ -180,12 +179,11 @@ def tile_multiheadlmattentionwithcache_pa_t_kernel(
             if half == 0:
                 st[("gv", b)] = w2.tile([P, H * D * 4], BF16, name="gv", tag="gv", align_bytes=64)
             gv = st[("gv", b)]
-            for h2 in range(2):
-                h = half * 2 + h2
-                nc.vector.tensor_copy(
-                    out=gv[:, h * 512:(h + 1) * 512].rearrange("p (c i j) -> p c j i", i=4, j=4),
-                    in_=vst[:, bb * H + h, :, :].rearrange("p j (c i) -> p c j i", i=4),
-                )
+            n0 = bb * H + half * 2
+            nc.vector.tensor_copy(
+                out=gv[:, half * 1024:(half + 1) * 1024].rearrange("p (h c i j) -> p h c j i", h=2, i=4, j=4),
+                in_=vst[:, n0:n0 + 2, :, :].rearrange("p h j (c i) -> p h c j i", i=4),
+            )
 
         def quant_v(b):
             vc = w3.tile([P, H * D], U32, name="vc", tag="vc", align_bytes=64)
@@ -235,8 +233,8 @@ def tile_multiheadlmattentionwithcache_pa_t_kernel(
             if qt == 0:
                 st[("nmax", g)] = w3.tile([P, 2], F32, name="nmax", tag="nmax")
                 st[("e", g)] = w4.tile([P, 896], BF16, name="e", tag="e")
-                if g % 2 == 0:
-                    st[("rsum", g // 2)] = w5.tile([P, 4], F32, name="rsum", tag="rsum")
+                if h == 0:
+                    st[("rsum", b)] = w3.tile([P, 2 * H], F32, name="rsum", tag="rsum")
             wd = 256 + qt * P
             wa = wd + P
             lq = qT[:, (h * 2 + qt) * P:(h * 2 + qt + 1) * P]
@@ -257,7 +255,7 @@ def tile_multiheadlmattentionwithcache_pa_t_kernel(
             nc.scalar.activation(
                 out=st[("e", g)][:, qt * 384:qt * 384 + wa], in_=st[("s", g, qt)][:, 0:wa], func=ACT.Exp,
                 bias=st[("nmax", g)][:, qt:qt + 1], scale=1.0,
-                accum_out=st[("rsum", g // 2)][:, (g % 2) * 2 + qt:(g % 2) * 2 + qt + 1],
+                accum_out=st[("rsum", g // H)][:, (g % H) * 2 + qt:(g % H) * 2 + qt + 1],
             )
 
         def et_t(g, qt):
@@ -301,10 +299,10 @@ def tile_multiheadlmattentionwithcache_pa_t_kernel(
             if h == 0:
                 st[("ob", b)] = w3.tile([P, 2, E], F32, name="ob", tag="ob")
             ob = st[("ob", b)]
-            if g % 2 == 0:
-                st[("rinv", g // 2)] = w3.tile([P, 4], F32, name="rinv", tag="rinv")
-                nc.vector.reciprocal(out=st[("rinv", g // 2)][:], in_=st[("rsum", g // 2)][:])
-            rinv = st[("rinv", g // 2)][:, (g % 2) * 2:(g % 2) * 2 + 2]
+            if h == 0:
+                st[("rinv", b)] = w2.tile([P, 2 * H], F32, name="rinv", tag="rinv")
+                nc.vector.reciprocal(out=st[("rinv", b)][:], in_=st[("rsum", b)][:])
+            rinv = st[("rinv", b)][:, h * 2:h * 2 + 2]
             nc.vector.tensor_tensor(
                 out=ob[:, :, h * D:(h + 1) * D], in0=st[("o", g)][:],
                 in1=rinv.unsqueeze(2).to_broadcast([P, 2, D]), op=ALU.mult,
@@ -336,7 +334,6 @@ def tile_multiheadlmattentionwithcache_pa_t_kernel(
                 on(b + 1, c_k, 1)
             head(k, sc_max, 0)
             head(k, sc_exp, 0)
-            head(k - 3, quant_e)
             if r == 0:
                 on(b + 1, pj_mm, 0)
             elif r == 1:
@@ -347,6 +344,7 @@ def tile_multiheadlmattentionwithcache_pa_t_kernel(
             head(k + 1, sc_mm, 0)
             head(k, sc_max, 1)
             head(k, sc_exp, 1)
+            head(k - 3, quant_e)
             head(k - 1, et_t, 1)
             head(k - 1, et_evac, 1)
             head(k - 4, pv_out)
@@ -360,11 +358,12 @@ def tile_multiheadlmattentionwithcache_pa_t_kernel(
                 on(b + 2, t_q)
             head(k + 1, sc_mm, 1)
             if r == 0:
-                on(b + 1, pj_add, 0)
                 on(b, quant_v)
+                on(b + 1, pj_add, 0)
+                on(b + 1, cast_v, 0)
             elif r == 1:
                 on(b + 1, pj_add, 1)
-                on(b + 1, cast_v)
+                on(b + 1, cast_v, 1)
             elif r == 2:
                 on(b + 1, regroup_v, 0)
             else:

@@ -18,10 +18,10 @@ P = 128
 NH = B * H
 FLOPS = 2 * T * B * E * E + 2 * 2 * NH * T * (C + T) * D
 
-NG = 4
+NG = 3
 CB = 2
 NCH = B // CB
-FIRST = -7
+FIRST = -8
 
 
 def tile_multiheadlmattentionwithcache_pa_t_kernel(
@@ -34,6 +34,7 @@ def tile_multiheadlmattentionwithcache_pa_t_kernel(
         w2 = ctx.enter_context(tc.tile_pool(name="w2", bufs=2))
         w3 = ctx.enter_context(tc.tile_pool(name="w3", bufs=3))
         w4 = ctx.enter_context(tc.tile_pool(name="w4", bufs=4))
+        w6 = ctx.enter_context(tc.tile_pool(name="w6", bufs=6))
         ps_s = ctx.enter_context(tc.psum_pool(name="ps_s", bufs=3))
         ps_e = ctx.enter_context(tc.psum_pool(name="ps_e", bufs=2))
         ps_m = ctx.enter_context(tc.psum_pool(name="ps_m", bufs=3))
@@ -59,8 +60,9 @@ def tile_multiheadlmattentionwithcache_pa_t_kernel(
             chunks[c] = (xs, qs, ks, cks, vst)
             wp = w // parts
             nh = CB * H // parts
+            nc.sync.dma_start(out=xs[:].rearrange("p (tt f) -> p tt f", tt=2), in_=x_v[:, :, c * w:(c + 1) * w])
             for i in range(parts):
-                for sb, dram in ((xs, x_v), (qs, q_v), (ks, k_v)):
+                for sb, dram in ((qs, q_v), (ks, k_v)):
                     nc.sync.dma_start(
                         out=sb[:].rearrange("p (tt f) -> p tt f", tt=2)[:, :, i * wp:(i + 1) * wp],
                         in_=dram[:, :, c * w + i * wp:c * w + (i + 1) * wp],
@@ -99,7 +101,7 @@ def tile_multiheadlmattentionwithcache_pa_t_kernel(
         nc.vector.tensor_copy(out=mask_b[:], in_=mask_f[:])
         gts = []
         for i in range(NG):
-            gt = const.tile([P, 2, P, 4], BF16, name="gt%d" % i, align_bytes=64)
+            gt = const.tile([P, 2, 2, P, 4], BF16, name="gt%d" % i, align_bytes=64)
             nc.vector.memset(gt[:], 0.0)
             gts.append(gt)
 
@@ -135,7 +137,7 @@ def tile_multiheadlmattentionwithcache_pa_t_kernel(
 
         def c_x(b):
             xg = w2.tile([P, 1024], BF16, name="xg", tag="xg", align_bytes=64)
-            nc.scalar.copy(
+            nc.vector.tensor_copy(
                 out=xg[:].bitcast(F32).rearrange("p (tt r u) -> p tt r u", tt=2, u=2),
                 in_=st[("xt", b)][:].rearrange("p tt u r -> p tt r u"),
             )
@@ -180,9 +182,10 @@ def tile_multiheadlmattentionwithcache_pa_t_kernel(
                 st[("gv", b)] = w2.tile([P, H * D * 4], BF16, name="gv", tag="gv", align_bytes=64)
             gv = st[("gv", b)]
             n0 = bb * H + half * 2
-            nc.vector.tensor_copy(
-                out=gv[:, half * 1024:(half + 1) * 1024].rearrange("p (h c i j) -> p h c j i", h=2, i=4, j=4),
-                in_=vst[:, n0:n0 + 2, :, :].rearrange("p h j (c i) -> p h c j i", i=4),
+            nc.gpsimd.tensor_scalar(
+                out=gv[:, half * 1024:(half + 1) * 1024].rearrange("p (h d j) -> p h d j", h=2, j=4),
+                in0=vst[:, n0:n0 + 2, :, :].rearrange("p h j d -> p h d j"),
+                scalar1=1.0, scalar2=0.0, op0=ALU.mult, op1=ALU.add,
             )
 
         def quant_v(b):
@@ -232,7 +235,7 @@ def tile_multiheadlmattentionwithcache_pa_t_kernel(
             k0 = (h % 2) * 512
             if qt == 0:
                 st[("nmax", g)] = w3.tile([P, 2], F32, name="nmax", tag="nmax")
-                st[("e", g)] = w4.tile([P, 896], BF16, name="e", tag="e")
+                st[("e", g)] = w6.tile([P, 896], BF16, name="e", tag="e")
                 if h == 0:
                     st[("rsum", b)] = w3.tile([P, 2 * H], F32, name="rsum", tag="rsum")
             wd = 256 + qt * P
@@ -258,58 +261,62 @@ def tile_multiheadlmattentionwithcache_pa_t_kernel(
                 accum_out=st[("rsum", g // H)][:, (g % H) * 2 + qt:(g % H) * 2 + qt + 1],
             )
 
-        def et_t(g, qt):
-            e = st[("e", g)]
-            et = ps_e.tile([P, 4, P], BF16, name="et", tag="et")
-            for j in range(3 + qt):
-                col = qt * 384 + j * P
-                nc.tensor.transpose(et[:, j, :], e[:, col:col + P], ident_b[:])
-            st[("et", g, qt)] = et
+        def et_t(mm, qt):
+            nj = 3 + qt
+            et = ps_e.tile([P, 2, nj, P], BF16, name="et", tag="et")
+            for h2 in range(2):
+                e = st[("e", 2 * mm + h2)]
+                for j in range(nj):
+                    col = qt * 384 + j * P
+                    nc.tensor.transpose(et[:, h2, j, :], e[:, col:col + P], ident_b[:])
+            st[("et", mm, qt)] = et
 
-        def et_evac(g, qt):
+        def et_evac(mm, qt):
             nj = 3 + qt
             nc.scalar.copy(
-                out=gts[g % NG][:, qt, :, 0:nj], in_=st[("et", g, qt)][:, 0:nj, :].rearrange("p j m -> p m j")
+                out=gts[mm % NG][:, :, qt, :, 0:nj], in_=st[("et", mm, qt)][:].rearrange("p h j m -> p h m j")
             )
 
-        def quant_e(g):
-            ec = w3.tile([P, 256], U32, name="ec", tag="ec", align_bytes=64)
-            esc = w3.tile([P, 256], U8, name="esc", tag="esc", align_bytes=64)
+        def quant_e(mm):
+            ec = w3.tile([P, 512], U32, name="ec", tag="ec", align_bytes=64)
+            esc = w3.tile([P, 512], U8, name="esc", tag="esc", align_bytes=64)
             nc.vector.quantize_mx(
-                out=ec[:].bitcast(FP8X4), scales=esc[:], in_=gts[g % NG][:].rearrange("p a m j -> p (a m j)")
+                out=ec[:].bitcast(FP8X4), scales=esc[:], in_=gts[mm % NG][:].rearrange("p h a m j -> p (h a m j)")
             )
-            st[("ec", g)] = (ec, esc)
+            st[("ec", mm)] = (ec, esc)
 
-        def pv_mm(g):
-            b, h = divmod(g, H)
-            ec, esc = st[("ec", g)]
+        def pv_mm(mm):
+            b, hp = divmod(mm, 2)
+            ec, esc = st[("ec", mm)]
             vc, vsc = st[("vc", b)]
-            o = ps_m.tile([P, 2, P], F32, name="o", tag="m")
-            for qt in range(2):
-                nc.tensor.matmul_mx(
-                    out=o[:, qt, :],
-                    lhsT=ec[:, qt * P:(qt + 1) * P].bitcast(FP8X4), lhsT_scale=esc[:, qt * P:(qt + 1) * P],
-                    rhs=vc[:, h * D:(h + 1) * D].bitcast(FP8X4), rhs_scale=vsc[:, h * D:(h + 1) * D],
-                    start=True, stop=True,
-                )
-            st[("o", g)] = o
+            o = ps_m.tile([P, 2, 2, P], F32, name="o", tag="m")
+            for h2 in range(2):
+                h = hp * 2 + h2
+                for qt in range(2):
+                    c0 = (h2 * 2 + qt) * P
+                    nc.tensor.matmul_mx(
+                        out=o[:, h2, qt, :],
+                        lhsT=ec[:, c0:c0 + P].bitcast(FP8X4), lhsT_scale=esc[:, c0:c0 + P],
+                        rhs=vc[:, h * D:(h + 1) * D].bitcast(FP8X4), rhs_scale=vsc[:, h * D:(h + 1) * D],
+                        start=True, stop=True,
+                    )
+            st[("o", mm)] = o
 
-        def pv_out(g):
-            b, h = divmod(g, H)
-            if h == 0:
+        def pv_out(mm):
+            b, hp = divmod(mm, 2)
+            if hp == 0:
                 st[("ob", b)] = w3.tile([P, 2, E], F32, name="ob", tag="ob")
-            ob = st[("ob", b)]
-            if h == 0:
                 st[("rinv", b)] = w2.tile([P, 2 * H], F32, name="rinv", tag="rinv")
                 nc.vector.reciprocal(out=st[("rinv", b)][:], in_=st[("rsum", b)][:])
-            rinv = st[("rinv", b)][:, h * 2:h * 2 + 2]
+            ob = st[("ob", b)]
+            rinv = st[("rinv", b)][:, hp * 4:hp * 4 + 4].rearrange("p (h a) -> p h a", h=2)
             nc.vector.tensor_tensor(
-                out=ob[:, :, h * D:(h + 1) * D], in0=st[("o", g)][:],
-                in1=rinv.unsqueeze(2).to_broadcast([P, 2, D]), op=ALU.mult,
+                out=ob[:, :, hp * 256:(hp + 1) * 256].rearrange("p a (h d) -> p h a d", h=2), in0=st[("o", mm)][:],
+                in1=rinv.unsqueeze(3).to_broadcast([P, 2, 2, D]), op=ALU.mult,
             )
             if b == B - 1:
-                nc.sync.dma_start(out=o0_v[:, :, b, h * D:(h + 1) * D], in_=ob[:, :, h * D:(h + 1) * D])
-            elif h == H - 1:
+                nc.sync.dma_start(out=o0_v[:, :, b, hp * 256:(hp + 1) * 256], in_=ob[:, :, hp * 256:(hp + 1) * 256])
+            elif hp == 1:
                 nc.sync.dma_start(out=o0_v[:, :, b, :], in_=ob[:])
 
         def on(batch, step, *args):
@@ -320,52 +327,53 @@ def tile_multiheadlmattentionwithcache_pa_t_kernel(
             if 0 <= g < NH:
                 step(g, *args)
 
+        def pair(mm, step, *args):
+            if 0 <= mm < NH // 2:
+                step(mm, *args)
+
         for k in range(FIRST, NH + 5):
             b, r = divmod(k, H)
+            m, odd = divmod(k, 2)
             if k >= 0 and k % (CB * H) == 0 and k // (CB * H) + 2 < NCH:
                 load_chunk(k // (CB * H) + 2, 1)
             if r == 0:
                 on(b + 1, c_q)
-            elif r == 1:
-                on(b + 1, c_k, 0)
             elif r == 2:
-                on(b + 2, c_x)
-            else:
+                on(b + 1, c_k, 0)
+            elif r == 3:
                 on(b + 1, c_k, 1)
             head(k, sc_max, 0)
             head(k, sc_exp, 0)
-            if r == 0:
-                on(b + 1, pj_mm, 0)
-            elif r == 1:
-                on(b + 1, pj_mm, 1)
-            head(k - 4, pv_mm)
-            head(k - 1, et_t, 0)
-            head(k - 1, et_evac, 0)
+            if odd:
+                pair(m - 2, pv_mm)
+            else:
+                on(b + 1, pj_mm, r // 2)
+            pair(m - 1, et_t, odd)
+            pair(m - 1, et_evac, odd)
             head(k + 1, sc_mm, 0)
             head(k, sc_max, 1)
             head(k, sc_exp, 1)
-            head(k - 3, quant_e)
-            head(k - 1, et_t, 1)
-            head(k - 1, et_evac, 1)
-            head(k - 4, pv_out)
+            if odd:
+                pair(m - 2, pv_out)
+                if r == 1:
+                    on(b + 2, c_x)
+            else:
+                pair(m - 2, quant_e)
+                if r == 2:
+                    on(b + 2, quant_x)
+                    on(b, quant_v)
+                on(b + 1, pj_add, r // 2)
+                on(b + 1, cast_v, r // 2)
+                if r == 0:
+                    on(b, regroup_v, 1)
+                else:
+                    on(b + 1, regroup_v, 0)
             if r == 0:
-                on(b + 1, t_k, 0)
-            elif r == 1:
                 on(b + 2, t_x)
+            elif r == 1:
+                on(b + 1, t_k, 0)
             elif r == 2:
                 on(b + 1, t_k, 1)
             else:
                 on(b + 2, t_q)
             head(k + 1, sc_mm, 1)
-            if r == 0:
-                on(b, quant_v)
-                on(b + 1, pj_add, 0)
-                on(b + 1, cast_v, 0)
-            elif r == 1:
-                on(b + 1, pj_add, 1)
-                on(b + 1, cast_v, 1)
-            elif r == 2:
-                on(b + 1, regroup_v, 0)
-            else:
-                on(b + 2, quant_x)
-                on(b + 1, regroup_v, 1)

@@ -19,6 +19,7 @@ NH = B * H
 FLOPS = 2 * T * B * E * E + 2 * 2 * NH * T * (C + T) * D
 
 NG = 3
+NE = 6
 CB = 2
 NCH = B // CB
 FIRST = -8
@@ -34,18 +35,17 @@ def tile_multiheadlmattentionwithcache_pa_t_kernel(
         w2 = ctx.enter_context(tc.tile_pool(name="w2", bufs=2))
         w3 = ctx.enter_context(tc.tile_pool(name="w3", bufs=3))
         w4 = ctx.enter_context(tc.tile_pool(name="w4", bufs=4))
-        w6 = ctx.enter_context(tc.tile_pool(name="w6", bufs=6))
         ps_s = ctx.enter_context(tc.psum_pool(name="ps_s", bufs=3))
         ps_e = ctx.enter_context(tc.psum_pool(name="ps_e", bufs=2))
         ps_m = ctx.enter_context(tc.psum_pool(name="ps_m", bufs=3))
 
-        x_v = x.rearrange("(tt p) b e -> p tt (b e)", p=P)
+        x_v = x.rearrange("(p tt) b e -> p tt (b e)", tt=2)
         q_v = q.rearrange("(tt p) b e -> p tt (b e)", p=P)
         k_v = k_new.rearrange("(tt p) b e -> p tt (b e)", p=P)
-        ck_v = cache_k.rearrange("n (p j) d -> p n (j d)", j=2)
+        ck_v = cache_k.rearrange("n c d -> (n c) d").rearrange("(a p) d -> p a d", p=P)
         cv_v = cache_v.rearrange("n (p j) d -> p n (j d)", j=2)
         o0_v = out_0.rearrange("(qt p) b e -> p qt b e", p=P)
-        o1_v = out_1.rearrange("(b h) (tt p) d -> p b tt h d", h=H, p=P)
+        o1_v = out_1.rearrange("(b h) (p tt) d -> p b tt h d", h=H, tt=2)
 
         chunks = {}
         st = {}
@@ -69,8 +69,8 @@ def tile_multiheadlmattentionwithcache_pa_t_kernel(
                     )
                 n0 = c * CB * H + i * nh
                 nc.sync.dma_start(
-                    out=cks[:].rearrange("p (n f) -> p n f", f=256)[:, i * nh:(i + 1) * nh, :],
-                    in_=ck_v[:, n0:n0 + nh, :],
+                    out=cks[:].rearrange("p (a d) -> p a d", d=D)[:, 2 * i * nh:2 * (i + 1) * nh, :],
+                    in_=ck_v[:, 2 * n0:2 * (n0 + nh), :],
                 )
                 nc.sync.dma_start(
                     out=vst[:].rearrange("p n j d -> p n (j d)")[:, i * nh:(i + 1) * nh, 0:256],
@@ -102,8 +102,12 @@ def tile_multiheadlmattentionwithcache_pa_t_kernel(
         gts = []
         for i in range(NG):
             gt = const.tile([P, 2, 2, P, 4], BF16, name="gt%d" % i, align_bytes=64)
-            nc.vector.memset(gt[:], 0.0)
             gts.append(gt)
+        es = []
+        for i in range(NE):
+            et0 = const.tile([P, 2, 512], BF16, name="e%d" % i)
+            nc.vector.memset(et0[:, 0, 384:512], 0.0)
+            es.append(et0)
 
         ctx.enter_context(tc.manual_schedule())
 
@@ -235,7 +239,7 @@ def tile_multiheadlmattentionwithcache_pa_t_kernel(
             k0 = (h % 2) * 512
             if qt == 0:
                 st[("nmax", g)] = w3.tile([P, 2], F32, name="nmax", tag="nmax")
-                st[("e", g)] = w6.tile([P, 896], BF16, name="e", tag="e")
+                st[("e", g)] = es[g % NE]
                 if h == 0:
                     st[("rsum", b)] = w3.tile([P, 2 * H], F32, name="rsum", tag="rsum")
             wd = 256 + qt * P
@@ -256,25 +260,22 @@ def tile_multiheadlmattentionwithcache_pa_t_kernel(
         def sc_exp(g, qt):
             wa = 384 + qt * P
             nc.scalar.activation(
-                out=st[("e", g)][:, qt * 384:qt * 384 + wa], in_=st[("s", g, qt)][:, 0:wa], func=ACT.Exp,
+                out=st[("e", g)][:, qt, 0:wa], in_=st[("s", g, qt)][:, 0:wa], func=ACT.Exp,
                 bias=st[("nmax", g)][:, qt:qt + 1], scale=1.0,
                 accum_out=st[("rsum", g // H)][:, (g % H) * 2 + qt:(g % H) * 2 + qt + 1],
             )
 
         def et_t(mm, qt):
-            nj = 3 + qt
-            et = ps_e.tile([P, 2, nj, P], BF16, name="et", tag="et")
+            et = ps_e.tile([P, 2, 2, P], F32, name="et", tag="et")
             for h2 in range(2):
-                e = st[("e", 2 * mm + h2)]
-                for j in range(nj):
-                    col = qt * 384 + j * P
-                    nc.tensor.transpose(et[:, h2, j, :], e[:, col:col + P], ident_b[:])
+                ew = st[("e", 2 * mm + h2)][:, qt, :].bitcast(F32)
+                for u in range(2):
+                    nc.tensor.transpose(et[:, h2, u, :], ew[:, u * P:(u + 1) * P], ident_f[:])
             st[("et", mm, qt)] = et
 
         def et_evac(mm, qt):
-            nj = 3 + qt
             nc.scalar.copy(
-                out=gts[mm % NG][:, :, qt, :, 0:nj], in_=st[("et", mm, qt)][:].rearrange("p h j m -> p h m j")
+                out=gts[mm % NG][:].bitcast(F32)[:, :, qt, :, :], in_=st[("et", mm, qt)][:].rearrange("p h u m -> p h m u")
             )
 
         def quant_e(mm):

@@ -141,7 +141,7 @@ def tile_multiheadlmattentionwithcache_pa_t_kernel(
 
         def c_x(b):
             xg = w2.tile([P, 1024], BF16, name="xg", tag="xg", align_bytes=64)
-            nc.vector.tensor_copy(
+            nc.scalar.copy(
                 out=xg[:].bitcast(F32).rearrange("p (tt r u) -> p tt r u", tt=2, u=2),
                 in_=st[("xt", b)][:].rearrange("p tt u r -> p tt r u"),
             )
@@ -339,6 +339,8 @@ def tile_multiheadlmattentionwithcache_pa_t_kernel(
                 load_chunk(k // (CB * H) + 2, 1)
             if r == 0:
                 on(b + 1, c_q)
+            elif r == 1:
+                on(b + 2, c_x)
             elif r == 2:
                 on(b + 1, c_k, 0)
             elif r == 3:
@@ -356,8 +358,6 @@ def tile_multiheadlmattentionwithcache_pa_t_kernel(
             head(k, sc_exp, 1)
             if odd:
                 pair(m - 2, pv_out)
-                if r == 1:
-                    on(b + 2, c_x)
             else:
                 pair(m - 2, quant_e)
                 if r == 2:

@@ -22,7 +22,6 @@ NG = 3
 NE = 6
 CB = 2
 NCH = B // CB
-FIRST = -8
 
 
 def tile_multiheadlmattentionwithcache_pa_t_kernel(
@@ -61,6 +60,8 @@ def tile_multiheadlmattentionwithcache_pa_t_kernel(
             wp = w // parts
             nh = CB * H // parts
             nc.sync.dma_start(out=xs[:].rearrange("p (tt f) -> p tt f", tt=2), in_=x_v[:, :, c * w:(c + 1) * w])
+            if c == 0:
+                nc.sync.dma_start(out=b_row[0:1, :], in_=bv.rearrange("(o e) -> o e", o=1))
             for i in range(parts):
                 for sb, dram in ((qs, q_v), (ks, k_v)):
                     nc.sync.dma_start(
@@ -77,13 +78,17 @@ def tile_multiheadlmattentionwithcache_pa_t_kernel(
                     in_=cv_v[:, n0:n0 + nh, :],
                 )
 
+        ctx.enter_context(tc.manual_schedule())
+
         b_row = const.tile([P, E], BF16, name="b_row")
         nc.vector.memset(b_row[:], 0.0)
-        nc.sync.dma_start(out=b_row[0:1, :], in_=bv.rearrange("(o e) -> o e", o=1))
-        ones_b = const.tile([P, P], BF16, name="ones_b")
-        nc.vector.memset(ones_b[:], 1.0)
         w_sb = const.tile([P, 4 * E], BF16, name="w_sb")
-        nc.sync.dma_start(out=w_sb[:].rearrange("p (ob k) -> p ob k", ob=4), in_=Wv.rearrange("(ob p) k -> p ob k", p=P))
+        w_hbm = Wv.rearrange("(ob p) k -> p ob k", p=P)
+        for half in range(2):
+            nc.sync.dma_start(
+                out=w_sb[:].rearrange("p (ob k) -> p ob k", ob=4)[:, 2 * half:2 * half + 2, :],
+                in_=w_hbm[:, 2 * half:2 * half + 2, :],
+            )
         load_chunk(0, CB)
         load_chunk(1, 1)
 
@@ -91,14 +96,14 @@ def tile_multiheadlmattentionwithcache_pa_t_kernel(
         make_identity(nc, ident_f[:])
         ident_b = const.tile([P, P], BF16, name="ident_b")
         make_identity(nc, ident_b[:])
+        ones_b = const.tile([P, P], BF16, name="ones_b")
+        nc.vector.memset(ones_b[:], 1.0)
         mask_f = const.tile([P, P], F32, name="mask_f")
         nc.gpsimd.memset(mask_f[:], 0.0)
         nc.gpsimd.affine_select(
             out=mask_f[:], in_=mask_f[:], compare_op=ALU.is_ge, fill=-1.0e10,
             base=0, pattern=[[-1, P]], channel_multiplier=1,
         )
-        mask_b = const.tile([P, P], BF16, name="mask_b")
-        nc.vector.tensor_copy(out=mask_b[:], in_=mask_f[:])
         gts = []
         for i in range(NG):
             gt = const.tile([P, 2, 2, P, 4], BF16, name="gt%d" % i, align_bytes=64)
@@ -108,26 +113,37 @@ def tile_multiheadlmattentionwithcache_pa_t_kernel(
             et0 = const.tile([P, 2, 512], BF16, name="e%d" % i)
             nc.vector.memset(et0[:, 0, 384:512], 0.0)
             es.append(et0)
-
-        ctx.enter_context(tc.manual_schedule())
+        mask_b = const.tile([P, P], BF16, name="mask_b")
+        nc.vector.tensor_copy(out=mask_b[:], in_=mask_f[:])
 
         w_w = w_sb[:].bitcast(F32)
         w_g = const.tile([P, 4 * E], BF16, name="w_g", align_bytes=64)
         w_gw = w_g[:].bitcast(F32).rearrange("p (ob o u) -> p ob o u", ob=4, u=2)
-        for half in range(2):
+        wc = const.tile([P, E], U32, name="wc", align_bytes=64)
+        wsc = const.tile([P, E], U8, name="wsc", align_bytes=64)
+        bias_f = const.tile([P, E], F32, name="bias_f")
+
+        def t_w(half):
             wt = ps_m.tile([P, 2, 2, P], F32, name="wt", tag="m")
             for o2 in range(2):
                 for u in range(2):
                     col = (half * 2 + o2) * 256 + u * P
                     nc.tensor.transpose(wt[:, o2, u, :], w_w[:, col:col + P], ident_f[:])
-            nc.vector.tensor_copy(out=w_gw[:, half * 2:half * 2 + 2], in_=wt[:].rearrange("p ob u o -> p ob o u"))
-        wc = const.tile([P, E], U32, name="wc", align_bytes=64)
-        wsc = const.tile([P, E], U8, name="wsc", align_bytes=64)
-        nc.vector.quantize_mx(out=wc[:].bitcast(FP8X4), scales=wsc[:], in_=w_g[:])
-        bias_ps = ps_m.tile([P, E], F32, name="bias_ps", tag="m")
-        nc.tensor.matmul(bias_ps[:], lhsT=ones_b[:], rhs=b_row[:], start=True, stop=True)
-        bias_f = const.tile([P, E], F32, name="bias_f")
-        nc.vector.tensor_copy(out=bias_f[:], in_=bias_ps[:])
+            st[("wt", half)] = wt
+
+        def c_w(half, copy):
+            copy(out=w_gw[:, half * 2:half * 2 + 2], in_=st[("wt", half)][:].rearrange("p ob u o -> p ob o u"))
+
+        def quant_w():
+            nc.vector.quantize_mx(out=wc[:].bitcast(FP8X4), scales=wsc[:], in_=w_g[:])
+
+        def bias_mm():
+            bias_ps = ps_m.tile([P, E], F32, name="bias_ps", tag="m")
+            nc.tensor.matmul(bias_ps[:], lhsT=ones_b[:], rhs=b_row[:], start=True, stop=True)
+            st["bias_ps"] = bias_ps
+
+        def c_bias():
+            nc.scalar.copy(out=bias_f[:], in_=st["bias_ps"][:])
 
         def t_x(b):
             c, bb = divmod(b, CB)
@@ -275,48 +291,54 @@ def tile_multiheadlmattentionwithcache_pa_t_kernel(
 
         def et_evac(mm, qt):
             nc.scalar.copy(
-                out=gts[mm % NG][:].bitcast(F32)[:, :, qt, :, :], in_=st[("et", mm, qt)][:].rearrange("p h u m -> p h m u")
+                out=gts[mm % NG][:].bitcast(F32)[:, qt, :, :, :], in_=st[("et", mm, qt)][:].rearrange("p h u m -> p h m u")
             )
 
-        def quant_e(mm):
-            ec = w3.tile([P, 512], U32, name="ec", tag="ec", align_bytes=64)
-            esc = w3.tile([P, 512], U8, name="esc", tag="esc", align_bytes=64)
+        def quant_e(mm, q0=0, nq=2):
+            if q0 == 0:
+                ec = w3.tile([P, 512], U32, name="ec", tag="ec", align_bytes=64)
+                esc = w3.tile([P, 512], U8, name="esc", tag="esc", align_bytes=64)
+                st[("ec", mm)] = (ec, esc)
+            ec, esc = st[("ec", mm)]
+            cols = slice(q0 * 256, (q0 + nq) * 256)
             nc.vector.quantize_mx(
-                out=ec[:].bitcast(FP8X4), scales=esc[:], in_=gts[mm % NG][:].rearrange("p h a m j -> p (h a m j)")
+                out=ec[:, cols].bitcast(FP8X4), scales=esc[:, cols],
+                in_=gts[mm % NG][:].rearrange("p a h m j -> p (a h m j)")[:, q0 * 1024:(q0 + nq) * 1024],
             )
-            st[("ec", mm)] = (ec, esc)
 
-        def pv_mm(mm):
+        def pv_mm(mm, q0=0, nq=2):
             b, hp = divmod(mm, 2)
             ec, esc = st[("ec", mm)]
             vc, vsc = st[("vc", b)]
             o = ps_m.tile([P, 2, 2, P], F32, name="o", tag="m")
-            for h2 in range(2):
-                h = hp * 2 + h2
-                for qt in range(2):
-                    c0 = (h2 * 2 + qt) * P
+            for qt in range(q0, q0 + nq):
+                for h2 in range(2):
+                    h = hp * 2 + h2
+                    c0 = (qt * 2 + h2) * P
                     nc.tensor.matmul_mx(
-                        out=o[:, h2, qt, :],
+                        out=o[:, qt, h2, :],
                         lhsT=ec[:, c0:c0 + P].bitcast(FP8X4), lhsT_scale=esc[:, c0:c0 + P],
                         rhs=vc[:, h * D:(h + 1) * D].bitcast(FP8X4), rhs_scale=vsc[:, h * D:(h + 1) * D],
                         start=True, stop=True,
                     )
             st[("o", mm)] = o
 
-        def pv_out(mm):
+        def pv_out(mm, q0=0, nq=2):
             b, hp = divmod(mm, 2)
+            tiles = slice(q0, q0 + nq)
+            cols = slice(hp * 256, (hp + 1) * 256)
             if hp == 0:
                 st[("ob", b)] = w3.tile([P, 2, E], F32, name="ob", tag="ob")
                 st[("rinv", b)] = w2.tile([P, 2 * H], F32, name="rinv", tag="rinv")
                 nc.vector.reciprocal(out=st[("rinv", b)][:], in_=st[("rsum", b)][:])
             ob = st[("ob", b)]
-            rinv = st[("rinv", b)][:, hp * 4:hp * 4 + 4].rearrange("p (h a) -> p h a", h=2)
+            rinv = st[("rinv", b)][:, hp * 4:hp * 4 + 4].rearrange("p (h a) -> p a h", h=2)[:, tiles, :]
             nc.vector.tensor_tensor(
-                out=ob[:, :, hp * 256:(hp + 1) * 256].rearrange("p a (h d) -> p h a d", h=2), in0=st[("o", mm)][:],
-                in1=rinv.unsqueeze(3).to_broadcast([P, 2, 2, D]), op=ALU.mult,
+                out=ob[:, tiles, cols].rearrange("p a (h d) -> p a h d", h=2), in0=st[("o", mm)][:, tiles, :, :],
+                in1=rinv.unsqueeze(3).to_broadcast([P, nq, 2, D]), op=ALU.mult,
             )
             if b == B - 1:
-                nc.sync.dma_start(out=o0_v[:, :, b, hp * 256:(hp + 1) * 256], in_=ob[:, :, hp * 256:(hp + 1) * 256])
+                nc.sync.dma_start(out=o0_v[:, tiles, b, cols], in_=ob[:, tiles, cols])
             elif hp == 1:
                 nc.sync.dma_start(out=o0_v[:, :, b, :], in_=ob[:])
 
@@ -332,7 +354,35 @@ def tile_multiheadlmattentionwithcache_pa_t_kernel(
             if 0 <= mm < NH // 2:
                 step(mm, *args)
 
-        for k in range(FIRST, NH + 5):
+        t_w(0)
+        t_w(1)
+        c_w(0, nc.scalar.copy)
+        c_w(1, nc.vector.tensor_copy)
+        t_x(0)
+        t_x(1)
+        c_x(0)
+        c_x(1)
+        quant_w()
+        bias_mm()
+        c_bias()
+        quant_x(0)
+        quant_x(1)
+        t_q(0)
+        c_q(0)
+        for tt in range(2):
+            pj_mm(0, tt)
+        for tt in range(2):
+            pj_add(0, tt)
+            cast_v(0, tt)
+        regroup_v(0, 0)
+        for hp in range(2):
+            t_k(0, hp)
+            c_k(0, hp)
+        sc_mm(0, 0)
+        t_q(1)
+        sc_mm(0, 1)
+
+        for k in range(NH):
             b, r = divmod(k, H)
             m, odd = divmod(k, 2)
             if k >= 0 and k % (CB * H) == 0 and k // (CB * H) + 2 < NCH:
@@ -378,3 +428,17 @@ def tile_multiheadlmattentionwithcache_pa_t_kernel(
             else:
                 on(b + 2, t_q)
             head(k + 1, sc_mm, 1)
+
+        last = NH // 2 - 1
+        et_t(last, 0)
+        et_evac(last, 0)
+        quant_e(last - 1)
+        et_t(last, 1)
+        et_evac(last, 1)
+        pv_mm(last - 1)
+        pv_out(last - 1)
+        for qt in range(2):
+            quant_e(last, qt, 1)
+        for qt in range(2):
+            pv_mm(last, qt, 1)
+            pv_out(last, qt, 1)

@@ -412,7 +412,10 @@ def tile_multiheadlmattentionwithcache_pa_t_kernel(
                 pair(m - 2, quant_e)
                 if r == 2:
                     on(b + 2, quant_x)
-                    on(b, quant_v)
+                    if b == B - 1:
+                        quant_v(b)
+                else:
+                    on(b - 1, quant_v)
                 on(b + 1, pj_add, r // 2)
                 on(b + 1, cast_v, r // 2)
                 if r == 0:

@@ -262,9 +262,8 @@ def tile_multiheadlmattentionwithcache_pa_t_kernel(
             wa = wd + P
             lq = qT[:, (h * 2 + qt) * P:(h * 2 + qt + 1) * P]
             s = ps_s.tile([P, 512], F32, name="s", tag="s")
-            nc.tensor.matmul(s[:, 0:wd], lhsT=lq, rhs=kT[:, k0:k0 + wd], start=True, stop=True)
-            nc.tensor.matmul(s[:, wd:wa], lhsT=ident_b[:], rhs=mask_b[:], start=True, stop=False)
-            nc.tensor.matmul(s[:, wd:wa], lhsT=lq, rhs=kT[:, k0 + wd:k0 + wa], start=False, stop=True)
+            nc.tensor.matmul(s[:, 0:wa], lhsT=lq, rhs=kT[:, k0:k0 + wa], start=True, stop=False)
+            nc.tensor.matmul(s[:, wd:wa], lhsT=ident_b[:], rhs=mask_b[:], start=False, stop=True)
             st[("s", g, qt)] = s
 
         def sc_max(g, qt):
@@ -403,6 +402,14 @@ def tile_multiheadlmattentionwithcache_pa_t_kernel(
                 on(b + 1, pj_mm, r // 2)
             pair(m - 1, et_t, odd)
             pair(m - 1, et_evac, odd)
+            if r == 0:
+                on(b + 2, t_x)
+            elif r == 1:
+                on(b + 1, t_k, 0)
+            elif r == 2:
+                on(b + 1, t_k, 1)
+            else:
+                on(b + 2, t_q)
             head(k + 1, sc_mm, 0)
             head(k, sc_max, 1)
             head(k, sc_exp, 1)
@@ -422,14 +429,6 @@ def tile_multiheadlmattentionwithcache_pa_t_kernel(
                     on(b, regroup_v, 1)
                 else:
                     on(b + 1, regroup_v, 0)
-            if r == 0:
-                on(b + 2, t_x)
-            elif r == 1:
-                on(b + 1, t_k, 0)
-            elif r == 2:
-                on(b + 1, t_k, 1)
-            else:
-                on(b + 2, t_q)
             head(k + 1, sc_mm, 1)
 
         last = NH // 2 - 1

@@ -49,7 +49,7 @@ def tile_multiheadlmattentionwithcache_pa_t_kernel(
         chunks = {}
         st = {}
 
-        def load_chunk(c, parts):
+        def new_chunk(c):
             w = CB * E
             xs = ld.tile([P, 2 * w], BF16, name="xs", tag="xs")
             qs = ld.tile([P, 2 * w], BF16, name="qs", tag="qs")
@@ -57,26 +57,34 @@ def tile_multiheadlmattentionwithcache_pa_t_kernel(
             cks = ld.tile([P, CB * H * 256], BF16, name="cks", tag="cks")
             vst = ld.tile([P, CB * H, 4, D], BF16, name="vst", tag="vst")
             chunks[c] = (xs, qs, ks, cks, vst)
-            wp = w // parts
-            nh = CB * H // parts
-            nc.sync.dma_start(out=xs[:].rearrange("p (tt f) -> p tt f", tt=2), in_=x_v[:, :, c * w:(c + 1) * w])
-            if c == 0:
-                nc.sync.dma_start(out=b_row[0:1, :], in_=bv.rearrange("(o e) -> o e", o=1))
-            for i in range(parts):
-                for sb, dram in ((qs, q_v), (ks, k_v)):
-                    nc.sync.dma_start(
-                        out=sb[:].rearrange("p (tt f) -> p tt f", tt=2)[:, :, i * wp:(i + 1) * wp],
-                        in_=dram[:, :, c * w + i * wp:c * w + (i + 1) * wp],
-                    )
-                n0 = c * CB * H + i * nh
-                nc.sync.dma_start(
-                    out=cks[:].rearrange("p (a d) -> p a d", d=D)[:, 2 * i * nh:2 * (i + 1) * nh, :],
-                    in_=ck_v[:, 2 * n0:2 * (n0 + nh), :],
-                )
-                nc.sync.dma_start(
-                    out=vst[:].rearrange("p n j d -> p n (j d)")[:, i * nh:(i + 1) * nh, 0:256],
-                    in_=cv_v[:, n0:n0 + nh, :],
-                )
+
+        def load_rows(c, which, b0, nb):
+            f0 = (c * CB + b0) * E
+            nc.sync.dma_start(
+                out=chunks[c][which][:].rearrange("p (tt f) -> p tt f", tt=2)[:, :, b0 * E:(b0 + nb) * E],
+                in_=(x_v, q_v, k_v)[which][:, :, f0:f0 + nb * E],
+            )
+
+        def load_cache_k(c, h0, nh):
+            n0 = c * CB * H + h0
+            nc.sync.dma_start(
+                out=chunks[c][3][:].rearrange("p (a d) -> p a d", d=D)[:, 2 * h0:2 * (h0 + nh), :],
+                in_=ck_v[:, 2 * n0:2 * (n0 + nh), :],
+            )
+
+        def load_cache_v(c, h0, nh):
+            n0 = c * CB * H + h0
+            nc.sync.dma_start(
+                out=chunks[c][4][:].rearrange("p n j d -> p n (j d)")[:, h0:h0 + nh, 0:256],
+                in_=cv_v[:, n0:n0 + nh, :],
+            )
+
+        def load_chunk(c):
+            new_chunk(c)
+            for which in range(3):
+                load_rows(c, which, 0, CB)
+            load_cache_k(c, 0, CB * H)
+            load_cache_v(c, 0, CB * H)
 
         ctx.enter_context(tc.manual_schedule())
 
@@ -89,8 +97,24 @@ def tile_multiheadlmattentionwithcache_pa_t_kernel(
                 out=w_sb[:].rearrange("p (ob k) -> p ob k", ob=4)[:, 2 * half:2 * half + 2, :],
                 in_=w_hbm[:, 2 * half:2 * half + 2, :],
             )
-        load_chunk(0, CB)
-        load_chunk(1, 1)
+        new_chunk(0)
+        new_chunk(1)
+        load_rows(0, 0, 0, CB)
+        nc.sync.dma_start(out=b_row[0:1, :], in_=bv.rearrange("(o e) -> o e", o=1))
+        load_rows(0, 1, 0, 1)
+        load_rows(0, 2, 0, 1)
+        load_cache_k(0, 0, 2)
+        load_cache_k(0, 2, 2)
+        load_cache_v(0, 0, H)
+        load_rows(0, 1, 1, 1)
+        load_rows(1, 0, 0, CB)
+        load_rows(0, 2, 1, 1)
+        load_cache_k(0, H, H)
+        load_cache_v(0, H, H)
+        load_rows(1, 1, 0, CB)
+        load_rows(1, 2, 0, CB)
+        load_cache_k(1, 0, CB * H)
+        load_cache_v(1, 0, CB * H)
 
         ident_f = const.tile([P, P], F32, name="ident_f")
         make_identity(nc, ident_f[:])
@@ -385,7 +409,7 @@ def tile_multiheadlmattentionwithcache_pa_t_kernel(
             b, r = divmod(k, H)
             m, odd = divmod(k, 2)
             if k >= 0 and k % (CB * H) == 0 and k // (CB * H) + 2 < NCH:
-                load_chunk(k // (CB * H) + 2, 1)
+                load_chunk(k // (CB * H) + 2)
             if r == 0:
                 on(b + 1, c_q)
             elif r == 1:

from contextlib import ExitStack

import concourse.mybir as mybir
from concourse.masks import make_identity

F32 = mybir.dt.float32
BF16 = mybir.dt.bfloat16
U32 = mybir.dt.uint32
U8 = mybir.dt.uint8
FP8X4 = mybir.dt.float8_e4m3fn_x4
ALU = mybir.AluOpType
ACT = mybir.ActivationFunctionType
AX = mybir.AxisListType

T, B, C, E, H = 256, 16, 256, 512, 4
D = 128
P = 128
NH = B * H
FLOPS = 2 * T * B * E * E + 2 * 2 * NH * T * (C + T) * D

NG = 3
NE = 6
CB = 2
NCH = B // CB


def tile_multiheadlmattentionwithcache_pa_t_kernel(
    tc, x, q, k_new, cache_k, cache_v, Wv, bv, out_0, out_1
):
    nc = tc.nc
    with ExitStack() as ctx:
        const = ctx.enter_context(tc.tile_pool(name="const", bufs=1))
        ld = ctx.enter_context(tc.tile_pool(name="ld", bufs=3))
        w2 = ctx.enter_context(tc.tile_pool(name="w2", bufs=2))
        w3 = ctx.enter_context(tc.tile_pool(name="w3", bufs=3))
        w4 = ctx.enter_context(tc.tile_pool(name="w4", bufs=4))
        ps_s = ctx.enter_context(tc.psum_pool(name="ps_s", bufs=3))
        ps_e = ctx.enter_context(tc.psum_pool(name="ps_e", bufs=2))
        ps_m = ctx.enter_context(tc.psum_pool(name="ps_m", bufs=3))

        x_v = x.rearrange("(p tt) b e -> p tt (b e)", tt=2)
        q_v = q.rearrange("(tt p) b e -> p tt (b e)", p=P)
        k_v = k_new.rearrange("(tt p) b e -> p tt (b e)", p=P)
        ck_v = cache_k.rearrange("n c d -> (n c) d").rearrange("(a p) d -> p a d", p=P)
        cv_v = cache_v.rearrange("n (p j) d -> p n (j d)", j=2)
        o0_v = out_0.rearrange("(qt p) b e -> p qt b e", p=P)
        o1_v = out_1.rearrange("(b h) (p tt) d -> p b tt h d", h=H, tt=2)

        chunks = {}
        st = {}

        def new_chunk(c):
            w = CB * E
            xs = ld.tile([P, 2 * w], BF16, name="xs", tag="xs")
            qs = ld.tile([P, 2 * w], BF16, name="qs", tag="qs")
            ks = ld.tile([P, 2 * w], BF16, name="ks", tag="ks")
            cks = ld.tile([P, CB * H * 256], BF16, name="cks", tag="cks")
            vst = ld.tile([P, CB * H, 4, D], BF16, name="vst", tag="vst")
            chunks[c] = (xs, qs, ks, cks, vst)

        def load_rows(c, which, b0, nb):
            f0 = (c * CB + b0) * E
            nc.sync.dma_start(
                out=chunks[c][which][:].rearrange("p (tt f) -> p tt f", tt=2)[:, :, b0 * E:(b0 + nb) * E],
                in_=(x_v, q_v, k_v)[which][:, :, f0:f0 + nb * E],
            )

        def load_cache_k(c, h0, nh):
            n0 = c * CB * H + h0
            nc.sync.dma_start(
                out=chunks[c][3][:].rearrange("p (a d) -> p a d", d=D)[:, 2 * h0:2 * (h0 + nh), :],
                in_=ck_v[:, 2 * n0:2 * (n0 + nh), :],
            )

        def load_cache_v(c, h0, nh):
            n0 = c * CB * H + h0
            nc.sync.dma_start(
                out=chunks[c][4][:].rearrange("p n j d -> p n (j d)")[:, h0:h0 + nh, 0:256],
                in_=cv_v[:, n0:n0 + nh, :],
            )

        def load_chunk(c):
            new_chunk(c)
            for which in range(3):
                load_rows(c, which, 0, CB)
            load_cache_k(c, 0, CB * H)
            load_cache_v(c, 0, CB * H)

        ctx.enter_context(tc.manual_schedule())

        b_row = const.tile([P, E], BF16, name="b_row")
        nc.vector.memset(b_row[:], 0.0)
        w_sb = const.tile([P, 4 * E], BF16, name="w_sb")
        w_hbm = Wv.rearrange("(ob p) k -> p ob k", p=P)
        for half in range(2):
            nc.sync.dma_start(
                out=w_sb[:].rearrange("p (ob k) -> p ob k", ob=4)[:, 2 * half:2 * half + 2, :],
                in_=w_hbm[:, 2 * half:2 * half + 2, :],
            )
        new_chunk(0)
        new_chunk(1)
        load_rows(0, 0, 0, CB)
        nc.sync.dma_start(out=b_row[0:1, :], in_=bv.rearrange("(o e) -> o e", o=1))
        load_rows(0, 1, 0, 1)
        load_rows(0, 2, 0, 1)
        load_cache_k(0, 0, 2)
        load_cache_k(0, 2, 2)
        load_cache_v(0, 0, H)
        load_rows(0, 1, 1, 1)
        load_rows(1, 0, 0, CB)
        load_rows(0, 2, 1, 1)
        load_cache_k(0, H, H)
        load_cache_v(0, H, H)
        load_rows(1, 1, 0, CB)
        load_rows(1, 2, 0, CB)
        load_cache_k(1, 0, CB * H)
        load_cache_v(1, 0, CB * H)

        ident_f = const.tile([P, P], F32, name="ident_f")
        make_identity(nc, ident_f[:])
        ident_b = const.tile([P, P], BF16, name="ident_b")
        make_identity(nc, ident_b[:])
        ones_b = const.tile([P, P], BF16, name="ones_b")
        nc.vector.memset(ones_b[:], 1.0)
        mask_f = const.tile([P, P], F32, name="mask_f")
        nc.gpsimd.memset(mask_f[:], 0.0)
        nc.gpsimd.affine_select(
            out=mask_f[:], in_=mask_f[:], compare_op=ALU.is_ge, fill=-1.0e10,
            base=0, pattern=[[-1, P]], channel_multiplier=1,
        )
        gts = []
        for i in range(NG):
            gt = const.tile([P, 2, 2, P, 4], BF16, name="gt%d" % i, align_bytes=64)
            gts.append(gt)
        es = []
        for i in range(NE):
            et0 = const.tile([P, 2, 512], BF16, name="e%d" % i)
            nc.vector.memset(et0[:, 0, 384:512], 0.0)
            es.append(et0)
        mask_b = const.tile([P, P], BF16, name="mask_b")
        nc.vector.tensor_copy(out=mask_b[:], in_=mask_f[:])

        w_w = w_sb[:].bitcast(F32)
        w_g = const.tile([P, 4 * E], BF16, name="w_g", align_bytes=64)
        w_gw = w_g[:].bitcast(F32).rearrange("p (ob o u) -> p ob o u", ob=4, u=2)
        wc = const.tile([P, E], U32, name="wc", align_bytes=64)
        wsc = const.tile([P, E], U8, name="wsc", align_bytes=64)
        bias_f = const.tile([P, E], F32, name="bias_f")

        def t_w(half):
            wt = ps_m.tile([P, 2, 2, P], F32, name="wt", tag="m")
            for o2 in range(2):
                for u in range(2):
                    col = (half * 2 + o2) * 256 + u * P
                    nc.tensor.transpose(wt[:, o2, u, :], w_w[:, col:col + P], ident_f[:])
            st[("wt", half)] = wt

        def c_w(half, copy):
            copy(out=w_gw[:, half * 2:half * 2 + 2], in_=st[("wt", half)][:].rearrange("p ob u o -> p ob o u"))

        def quant_w():
            nc.vector.quantize_mx(out=wc[:].bitcast(FP8X4), scales=wsc[:], in_=w_g[:])

        def bias_mm():
            bias_ps = ps_m.tile([P, E], F32, name="bias_ps", tag="m")
            nc.tensor.matmul(bias_ps[:], lhsT=ones_b[:], rhs=b_row[:], start=True, stop=True)
            st["bias_ps"] = bias_ps

        def c_bias():
            nc.scalar.copy(out=bias_f[:], in_=st["bias_ps"][:])

        def t_x(b):
            c, bb = divmod(b, CB)
            xw = chunks[c][0][:].bitcast(F32)
            xt = ps_m.tile([P, 2, 2, P], F32, name="xt", tag="m")
            for tt in range(2):
                for u in range(2):
                    col = tt * (CB * 256) + bb * 256 + u * P
                    nc.tensor.transpose(xt[:, tt, u, :], xw[:, col:col + P], ident_f[:])
            st[("xt", b)] = xt

        def c_x(b):
            xg = w2.tile([P, 1024], BF16, name="xg", tag="xg", align_bytes=64)
            nc.scalar.copy(
                out=xg[:].bitcast(F32).rearrange("p (tt r u) -> p tt r u", tt=2, u=2),
                in_=st[("xt", b)][:].rearrange("p tt u r -> p tt r u"),
            )
            st[("xg", b)] = xg

        def quant_x(b):
            xc = w2.tile([P, 256], U32, name="xc", tag="xc", align_bytes=64)
            xsc = w2.tile([P, 256], U8, name="xsc", tag="xsc", align_bytes=64)
            nc.vector.quantize_mx(out=xc[:].bitcast(FP8X4), scales=xsc[:], in_=st[("xg", b)][:])
            st[("xc", b)] = (xc, xsc)
            st[("vh", b)] = w2.tile([P, 2, E], F32, name="vh", tag="vh")

        def pj_mm(b, tt):
            xc, xsc = st[("xc", b)]
            pp = ps_m.tile([P, E], F32, name="pp", tag="m")
            nc.tensor.matmul_mx(
                out=pp[:],
                lhsT=xc[:, tt * P:(tt + 1) * P].bitcast(FP8X4), lhsT_scale=xsc[:, tt * P:(tt + 1) * P],
                rhs=wc[:].bitcast(FP8X4), rhs_scale=wsc[:],
                start=True, stop=True,
            )
            st[("pp", b, tt)] = pp

        def pj_add(b, tt):
            vh = st[("vh", b)]
            nc.vector.tensor_tensor(out=vh[:, tt, :], in0=st[("pp", b, tt)][:], in1=bias_f[:], op=ALU.add)
            nc.sync.dma_start(out=o1_v[:, b, tt], in_=vh[:, tt, :].rearrange("p (h d) -> p h d", h=H))

        def cast_v(b, tt):
            c, bb = divmod(b, CB)
            vst = chunks[c][4]
            nc.gpsimd.tensor_scalar(
                out=vst[:, bb * H:(bb + 1) * H, 2 + tt, :],
                in0=st[("vh", b)][:, tt, :].rearrange("p (h d) -> p h d", h=H),
                scalar1=1.0, scalar2=0.0, op0=ALU.mult, op1=ALU.add,
            )

        def regroup_v(b, half):
            c, bb = divmod(b, CB)
            vst = chunks[c][4]
            if half == 0:
                st[("gv", b)] = w2.tile([P, H * D * 4], BF16, name="gv", tag="gv", align_bytes=64)
            gv = st[("gv", b)]
            n0 = bb * H + half * 2
            nc.gpsimd.tensor_scalar(
                out=gv[:, half * 1024:(half + 1) * 1024].rearrange("p (h d j) -> p h d j", h=2, j=4),
                in0=vst[:, n0:n0 + 2, :, :].rearrange("p h j d -> p h d j"),
                scalar1=1.0, scalar2=0.0, op0=ALU.mult, op1=ALU.add,
            )

        def quant_v(b):
            vc = w3.tile([P, H * D], U32, name="vc", tag="vc", align_bytes=64)
            vsc = w3.tile([P, H * D], U8, name="vsc", tag="vsc", align_bytes=64)
            nc.vector.quantize_mx(out=vc[:].bitcast(FP8X4), scales=vsc[:], in_=st[("gv", b)][:])
            st[("vc", b)] = (vc, vsc)

        def t_q(b):
            c, bb = divmod(b, CB)
            qs = chunks[c][1]
            tp = ps_m.tile([P, 8, P], BF16, name="tq", tag="m")
            for h in range(H):
                for tt in range(2):
                    col = tt * (CB * E) + bb * E + h * D
                    nc.tensor.transpose(tp[:, h * 2 + tt, :], qs[:, col:col + D], ident_b[:])
            st[("tq", b)] = tp

        def c_q(b):
            qT = w2.tile([P, 8 * P], BF16, name="qT", tag="qT")
            nc.scalar.copy(out=qT[:], in_=st[("tq", b)][:].rearrange("p a m -> p (a m)"))
            st[("qT", b)] = qT

        def t_k(b, hp):
            c, bb = divmod(b, CB)
            ks, cks = chunks[c][2], chunks[c][3]
            tp = ps_m.tile([P, 8, P], BF16, name="tk", tag="m")
            for h2 in range(2):
                h = hp * 2 + h2
                for j in range(2):
                    col = (bb * H + h) * 256 + j * D
                    nc.tensor.transpose(tp[:, h2 * 4 + j, :], cks[:, col:col + D], ident_b[:])
                for tt in range(2):
                    col = tt * (CB * E) + bb * E + h * D
                    nc.tensor.transpose(tp[:, h2 * 4 + 2 + tt, :], ks[:, col:col + D], ident_b[:])
            st[("tk", b, hp)] = tp

        def c_k(b, hp):
            kT = w4.tile([P, 8 * P], BF16, name="kT", tag="kT")
            nc.scalar.copy(out=kT[:], in_=st[("tk", b, hp)][:].rearrange("p a m -> p (a m)"))
            st[("kT", b, hp)] = kT

        def sc_mm(g, qt):
            b, h = divmod(g, H)
            qT = st[("qT", b)]
            kT = st[("kT", b, h // 2)]
            k0 = (h % 2) * 512
            if qt == 0:
                st[("nmax", g)] = w3.tile([P, 2], F32, name="nmax", tag="nmax")
                st[("e", g)] = es[g % NE]
                if h == 0:
                    st[("rsum", b)] = w3.tile([P, 2 * H], F32, name="rsum", tag="rsum")
            wd = 256 + qt * P
            wa = wd + P
            lq = qT[:, (h * 2 + qt) * P:(h * 2 + qt + 1) * P]
            s = ps_s.tile([P, 512], F32, name="s", tag="s")
            nc.tensor.matmul(s[:, 0:wa], lhsT=lq, rhs=kT[:, k0:k0 + wa], start=True, stop=False)
            nc.tensor.matmul(s[:, wd:wa], lhsT=ident_b[:], rhs=mask_b[:], start=False, stop=True)
            st[("s", g, qt)] = s

        def sc_max(g, qt):
            wa = 384 + qt * P
            nc.vector.tensor_reduce(
                out=st[("nmax", g)][:, qt:qt + 1], in_=st[("s", g, qt)][:, 0:wa], axis=AX.X, op=ALU.max, negate=True
            )

        def sc_exp(g, qt):
            wa = 384 + qt * P
            nc.scalar.activation(
                out=st[("e", g)][:, qt, 0:wa], in_=st[("s", g, qt)][:, 0:wa], func=ACT.Exp,
                bias=st[("nmax", g)][:, qt:qt + 1], scale=1.0,
                accum_out=st[("rsum", g // H)][:, (g % H) * 2 + qt:(g % H) * 2 + qt + 1],
            )

        def et_t(mm, qt):
            et = ps_e.tile([P, 2, 2, P], F32, name="et", tag="et")
            for h2 in range(2):
                ew = st[("e", 2 * mm + h2)][:, qt, :].bitcast(F32)
                for u in range(2):
                    nc.tensor.transpose(et[:, h2, u, :], ew[:, u * P:(u + 1) * P], ident_f[:])
            st[("et", mm, qt)] = et

        def et_evac(mm, qt):
            nc.scalar.copy(
                out=gts[mm % NG][:].bitcast(F32)[:, qt, :, :, :], in_=st[("et", mm, qt)][:].rearrange("p h u m -> p h m u")
            )

        def quant_e(mm, q0=0, nq=2):
            if q0 == 0:
                ec = w3.tile([P, 512], U32, name="ec", tag="ec", align_bytes=64)
                esc = w3.tile([P, 512], U8, name="esc", tag="esc", align_bytes=64)
                st[("ec", mm)] = (ec, esc)
            ec, esc = st[("ec", mm)]
            cols = slice(q0 * 256, (q0 + nq) * 256)
            nc.vector.quantize_mx(
                out=ec[:, cols].bitcast(FP8X4), scales=esc[:, cols],
                in_=gts[mm % NG][:].rearrange("p a h m j -> p (a h m j)")[:, q0 * 1024:(q0 + nq) * 1024],
            )

        def pv_mm(mm, q0=0, nq=2):
            b, hp = divmod(mm, 2)
            ec, esc = st[("ec", mm)]
            vc, vsc = st[("vc", b)]
            o = ps_m.tile([P, 2, 2, P], F32, name="o", tag="m")
            for qt in range(q0, q0 + nq):
                for h2 in range(2):
                    h = hp * 2 + h2
                    c0 = (qt * 2 + h2) * P
                    nc.tensor.matmul_mx(
                        out=o[:, qt, h2, :],
                        lhsT=ec[:, c0:c0 + P].bitcast(FP8X4), lhsT_scale=esc[:, c0:c0 + P],
                        rhs=vc[:, h * D:(h + 1) * D].bitcast(FP8X4), rhs_scale=vsc[:, h * D:(h + 1) * D],
                        start=True, stop=True,
                    )
            st[("o", mm)] = o

        def pv_out(mm, q0=0, nq=2):
            b, hp = divmod(mm, 2)
            tiles = slice(q0, q0 + nq)
            cols = slice(hp * 256, (hp + 1) * 256)
            if hp == 0:
                st[("ob", b)] = w3.tile([P, 2, E], F32, name="ob", tag="ob")
                st[("rinv", b)] = w2.tile([P, 2 * H], F32, name="rinv", tag="rinv")
                nc.vector.reciprocal(out=st[("rinv", b)][:], in_=st[("rsum", b)][:])
            ob = st[("ob", b)]
            rinv = st[("rinv", b)][:, hp * 4:hp * 4 + 4].rearrange("p (h a) -> p a h", h=2)[:, tiles, :]
            nc.vector.tensor_tensor(
                out=ob[:, tiles, cols].rearrange("p a (h d) -> p a h d", h=2), in0=st[("o", mm)][:, tiles, :, :],
                in1=rinv.unsqueeze(3).to_broadcast([P, nq, 2, D]), op=ALU.mult,
            )
            if b == B - 1:
                nc.sync.dma_start(out=o0_v[:, tiles, b, cols], in_=ob[:, tiles, cols])
            elif hp == 1:
                nc.sync.dma_start(out=o0_v[:, :, b, :], in_=ob[:])

        def on(batch, step, *args):
            if 0 <= batch < B:
                step(batch, *args)

        def head(g, step, *args):
            if 0 <= g < NH:
                step(g, *args)

        def pair(mm, step, *args):
            if 0 <= mm < NH // 2:
                step(mm, *args)

        t_w(0)
        t_w(1)
        c_w(0, nc.scalar.copy)
        c_w(1, nc.vector.tensor_copy)
        t_x(0)
        t_x(1)
        c_x(0)
        c_x(1)
        quant_w()
        bias_mm()
        c_bias()
        quant_x(0)
        quant_x(1)
        t_q(0)
        c_q(0)
        for tt in range(2):
            pj_mm(0, tt)
        for tt in range(2):
            pj_add(0, tt)
            cast_v(0, tt)
        regroup_v(0, 0)
        for hp in range(2):
            t_k(0, hp)
            c_k(0, hp)
        sc_mm(0, 0)
        t_q(1)
        sc_mm(0, 1)

        for k in range(NH):
            b, r = divmod(k, H)
            m, odd = divmod(k, 2)
            if k >= 0 and k % (CB * H) == 0 and k // (CB * H) + 2 < NCH:
                load_chunk(k // (CB * H) + 2)
            if r == 0:
                on(b + 1, c_q)
            elif r == 1:
                on(b + 2, c_x)
            elif r == 2:
                on(b + 1, c_k, 0)
            elif r == 3:
                on(b + 1, c_k, 1)
            head(k, sc_max, 0)
            head(k, sc_exp, 0)
            if odd:
                pair(m - 2, pv_mm)
            else:
                on(b + 1, pj_mm, r // 2)
            pair(m - 1, et_t, odd)
            pair(m - 1, et_evac, odd)
            if r == 0:
                on(b + 2, t_x)
            elif r == 1:
                on(b + 1, t_k, 0)
            elif r == 2:
                on(b + 1, t_k, 1)
            else:
                on(b + 2, t_q)
            head(k + 1, sc_mm, 0)
            head(k, sc_max, 1)
            head(k, sc_exp, 1)
            if odd:
                pair(m - 2, pv_out)
            else:
                pair(m - 2, quant_e)
                if r == 2:
                    on(b + 2, quant_x)
                    if b == B - 1:
                        quant_v(b)
                else:
                    on(b - 1, quant_v)
                on(b + 1, pj_add, r // 2)
                on(b + 1, cast_v, r // 2)
                if r == 0:
                    on(b, regroup_v, 1)
                else:
                    on(b + 1, regroup_v, 0)
            head(k + 1, sc_mm, 1)

        last = NH // 2 - 1
        et_t(last, 0)
        et_evac(last, 0)
        quant_e(last - 1)
        et_t(last, 1)
        et_evac(last, 1)
        pv_mm(last - 1)
        pv_out(last - 1)
        for qt in range(2):
            quant_e(last, qt, 1)
        for qt in range(2):
            pv_mm(last, qt, 1)
            pv_out(last, qt, 1)
